import numpy as np
import ml_dtypes


def mxq(x, axis, fmt="e4m3"):
    dtype, down = {"e4m3": (ml_dtypes.float8_e4m3fn, 7), "e5m2": (ml_dtypes.float8_e5m2, 14)}[fmt]
    v = np.moveaxis(np.asarray(x, np.float32).astype(ml_dtypes.bfloat16).astype(np.float64), axis, -1)
    blocks = v.reshape(v.shape[:-1] + (-1, 32))
    amax = np.abs(blocks).max(-1, keepdims=True)
    byte = np.maximum(np.where(amax > 0, np.frexp(amax)[1] - 1 + 127, 0) - down, 1)
    scale = np.exp2(byte - 127.0)
    codes = (blocks / scale).astype(np.float32).astype(dtype).astype(np.float64)
    return np.moveaxis((codes * scale).reshape(v.shape), -1, axis)


WIDE = False


def mx_kscale(k):
    if not WIDE:
        return np.ones(k)
    levels = np.array([10, -10, 5, -5, 0])
    a = np.random.permutation(np.resize(levels, k // 512 * 4)).reshape(k // 512, 4)
    idx = np.arange(k)
    return np.exp2(a[idx // 512, idx % 128 // 32])


BF16 = ml_dtypes.bfloat16


def bf(x):
    return np.asarray(x, np.float32).astype(BF16)


def f64(x):
    return np.asarray(x).astype(np.float64)


B, EMBED, DETER, STOC, HID, ACT = 4096, 512, 512, 64, 512, 12
DIST = 2 * STOC
CAT = DETER + EMBED


def softplus(v):
    return np.maximum(v, 0.0) + np.log(1.0 + np.exp(-np.abs(v)))


def setup_inputs():
    s = mx_kscale(CAT)
    tp, tq = mx_kscale(HID), mx_kscale(HID)
    r = np.random.standard_normal
    return {
        "h": bf(r((B, DETER)) * 0.65 * s[:DETER]),
        "embedding": bf(r((B, EMBED)) * s[DETER:]),
        "wp1": bf(r((HID, DETER)) / np.sqrt(DETER) / s[:DETER] * tp[:, None]),
        "bp1": bf(r(HID) * 0.1 * tp),
        "wp2": bf(r((DIST, HID)) / np.sqrt(HID) / tp),
        "bp2": bf(r(DIST) * 0.1),
        "wq1": bf(r((HID, CAT)) / np.sqrt(CAT) / s * tq[:, None]),
        "bq1": bf(r(HID) * 0.1 * tq),
        "wq2": bf(r((DIST, HID)) / np.sqrt(HID) / tq),
        "bq2": bf(r(DIST) * 0.1),
    }


def reference(h, embedding, wp1, bp1, wp2, bp2, wq1, bq1, wq2, bq2):
    cq = mxq(np.concatenate([f64(h), f64(embedding)], -1), 1, "e4m3")
    ap = np.maximum((cq[:, :DETER] @ mxq(f64(wp1), 1, "e4m3").T) + f64(bp1), 0.0)
    prior = (mxq(ap, 1, "e4m3") @ mxq(f64(wp2), 1, "e4m3").T) + f64(bp2)
    prior_mean, prior_std = np.split(prior, 2, axis=-1)
    prior_std = softplus(prior_std) + 0.1
    aq = np.maximum((cq @ mxq(f64(wq1), 1, "e4m3").T) + f64(bq1), 0.0)
    post = (mxq(aq, 1, "e4m3") @ mxq(f64(wq2), 1, "e4m3").T) + f64(bq2)
    post_mean, post_std = np.split(post, 2, axis=-1)
    post_std = softplus(post_std) + 0.1
    return (post_mean, post_std, prior_mean, prior_std)

@@ -1,0 +1,339 @@
+from contextlib import ExitStack
+
+import concourse.mybir as mybir
+from concourse.masks import make_identity
+
+F32 = mybir.dt.float32
+BF16 = mybir.dt.bfloat16
+U32 = mybir.dt.uint32
+U8 = mybir.dt.uint8
+FP8X4 = mybir.dt.float8_e4m3fn_x4
+ACT = mybir.ActivationFunctionType
+ALU = mybir.AluOpType
+
+P = 128
+PACK = 4
+K_PASS = P * PACK
+WORDS = K_PASS // 2
+
+BATCH = 4096
+HID = 512
+DIST = 128
+STOC = DIST // 2
+CHUNKS = HID // P
+
+ROWS = BATCH // P
+TILES = 4
+GROUP = TILES * P
+GROUPS = ROWS // TILES
+
+PRIOR, POST = 0, 1
+STEPS = 2 * GROUPS
+
+FLOPS = 2 * BATCH * (HID * K_PASS + HID * 2 * K_PASS + 2 * DIST * HID)
+
+
+def tile_rssmcell_pb_t_kernel(
+    tc, h, embedding, wp1, bp1, wp2, bp2, wq1, bq1, wq2, bq2, out_0, out_1, out_2, out_3
+):
+    nc = tc.nc
+    with ExitStack() as ctx:
+        keep = ctx.enter_context(tc.tile_pool(name="keep", bufs=1))
+        raw = ctx.enter_context(tc.tile_pool(name="raw", bufs=GROUPS))
+        stage = ctx.enter_context(tc.tile_pool(name="stage", bufs=3))
+        quantised = ctx.enter_context(tc.tile_pool(name="quantised", bufs=4))
+        psum_t = ctx.enter_context(tc.psum_pool(name="psum_t", bufs=2))
+        psum_first = ctx.enter_context(tc.psum_pool(name="psum_first", bufs=5))
+        psum_second = ctx.enter_context(tc.psum_pool(name="psum_second", bufs=1))
+        ctx.enter_context(tc.manual_schedule())
+
+        ident_f32 = keep.tile([P, P], F32)
+        make_identity(nc, ident_f32[:])
+        ident_bf16 = keep.tile([P, P], BF16)
+        make_identity(nc, ident_bf16[:])
+        ones = keep.tile([P, P], BF16)
+        nc.vector.memset(ones[:], 1.0)
+        one_column = keep.tile([P, 1], F32)
+        nc.vector.memset(one_column[:], 1.0)
+        bias1_rows = keep.tile([P, P], BF16)
+        nc.vector.memset(bias1_rows[:], 0.0)
+        bias2_row = keep.tile([P, 2 * DIST], BF16)
+        nc.vector.memset(bias2_row[:], 0.0)
+
+        h_rows = h.rearrange("(p j) k -> p j k", j=ROWS)
+        e_rows = embedding.rearrange("(p j) k -> p j k", j=ROWS)
+
+        def load_group(rows, g, name):
+            tile = raw.tile([P, TILES, K_PASS], BF16, name=name)
+            nc.sync.dma_start(out=tile[:], in_=rows[:, g * TILES : (g + 1) * TILES, :])
+            return tile
+
+        wp1_raw = keep.tile([P, CHUNKS, K_PASS], BF16)
+        nc.sync.dma_start(out=wp1_raw[:], in_=wp1.rearrange("(t p) k -> p t k", p=P))
+        h_raw = [load_group(h_rows, 0, "h_raw")]
+        nc.sync.dma_start(out=bias1_rows[0:CHUNKS, :], in_=bp1.rearrange("(t p) -> t p", p=P))
+        nc.sync.dma_start(
+            out=bias1_rows[CHUNKS : 2 * CHUNKS, :], in_=bq1.rearrange("(t p) -> t p", p=P)
+        )
+        wq1_raw = keep.tile([P, CHUNKS, 2 * K_PASS], BF16)
+        nc.sync.dma_start(out=wq1_raw[:], in_=wq1.rearrange("(t p) k -> p t k", p=P))
+        e_raw = [load_group(e_rows, 0, "e_raw")]
+        w2_raw = []
+        for head, w2 in ((PRIOR, wp2), (POST, wq2)):
+            tile = keep.tile([P, HID], BF16, name="w2_raw%d" % head)
+            nc.sync.dma_start(out=tile[:], in_=w2)
+            w2_raw.append(tile)
+        nc.sync.dma_start(out=bias2_row[0:1, 0:DIST], in_=bp2.rearrange("(o d) -> o d", o=1))
+        nc.sync.dma_start(
+            out=bias2_row[0:1, DIST : 2 * DIST], in_=bq2.rearrange("(o d) -> o d", o=1)
+        )
+        for g in range(1, GROUPS):
+            h_raw.append(load_group(h_rows, g, "h_raw"))
+            e_raw.append(load_group(e_rows, g, "e_raw"))
+
+        w1_codes = [
+            keep.tile([P, 1, HID], U32, name="wp1_codes", align_bytes=64),
+            keep.tile([P, 2, HID], U32, name="wq1_codes", align_bytes=64),
+        ]
+        w1_scales = [
+            keep.tile([P, 1, HID], U8, name="wp1_scales", align_bytes=64),
+            keep.tile([P, 2, HID], U8, name="wq1_scales", align_bytes=64),
+        ]
+        wq1_words = wq1_raw[:].bitcast(F32)
+        operand_passes = [
+            (wp1_raw[:].bitcast(F32), w1_codes[PRIOR][:, 0, :], w1_scales[PRIOR][:, 0, :]),
+            (h_raw[0][:].bitcast(F32), None, None),
+            (wq1_words[:, :, 0:WORDS], w1_codes[POST][:, 0, :], w1_scales[POST][:, 0, :]),
+            (wq1_words[:, :, WORDS : 2 * WORDS], w1_codes[POST][:, 1, :], w1_scales[POST][:, 1, :]),
+            (e_raw[0][:].bitcast(F32), None, None),
+        ]
+        for g in range(1, GROUPS):
+            operand_passes.append((h_raw[g][:].bitcast(F32), None, None))
+            operand_passes.append((e_raw[g][:].bitcast(F32), None, None))
+        FIRST_IN_LOOP = 5
+
+        def pass_of(source, g):
+            if g == 0:
+                return 1 if source == 0 else 4
+            return FIRST_IN_LOOP + 2 * (g - 1) + source
+
+        grouped_of = {}
+        banks_of = {}
+        operand_of = {}
+
+        def transpose_pass(n):
+            words = operand_passes[n][0]
+            banks = []
+            for half in range(2):
+                bank = psum_t.tile([P, 2, 2 * P], F32, name="bank")
+                for r in range(2):
+                    for u in range(2):
+                        nc.tensor.transpose(
+                            bank[:, u, r * P : (r + 1) * P],
+                            words[:, 2 * half + r, u * P : (u + 1) * P],
+                            ident_f32[:],
+                        )
+                banks.append(bank)
+            banks_of[n] = banks
+            grouped_of[n] = stage.tile([P, GROUP, PACK], BF16, name="grouped", align_bytes=64)
+
+        def empty_bank(n, half):
+            out = grouped_of[n][:].bitcast(F32)[:, half * 2 * P : (half + 1) * 2 * P, :]
+            in_ = banks_of[n][half][:].rearrange("p u c -> p c u")
+            if half == 0:
+                nc.scalar.copy(out=out, in_=in_)
+            else:
+                nc.vector.tensor_copy(out=out, in_=in_)
+
+        def quantise_pass(n):
+            codes, scales = operand_passes[n][1], operand_passes[n][2]
+            if codes is None:
+                codes = quantised.tile([P, GROUP], U32, name="c_codes", align_bytes=64)[:]
+                scales = quantised.tile([P, GROUP], U8, name="c_scales", align_bytes=64)[:]
+            nc.vector.quantize_mx(
+                out=codes.bitcast(FP8X4),
+                scales=scales,
+                in_=grouped_of[n][:].rearrange("p c t -> p (c t)"),
+            )
+            operand_of[n] = (codes, scales)
+
+        bias1 = keep.tile([P, 2 * CHUNKS], F32)
+
+        def first_layer_bank(step, t):
+            g, head = divmod(step, 2)
+            bank = psum_first.tile([P, GROUP], F32, name="hidden_bank")
+            units = slice(t * P, (t + 1) * P)
+            passes = 1 + head
+            for c in range(passes):
+                codes, scales = operand_of[pass_of(c, g)]
+                nc.tensor.matmul_mx(
+                    out=bank[:],
+                    lhsT=w1_codes[head][:, c, units].bitcast(FP8X4),
+                    lhsT_scale=w1_scales[head][:, c, units],
+                    rhs=codes.bitcast(FP8X4),
+                    rhs_scale=scales,
+                    start=(c == 0),
+                    stop=(c == passes - 1),
+                )
+            return bank
+
+        def relu_out(step, t, bank, hidden):
+            column = CHUNKS * (step % 2) + t
+            nc.scalar.activation(
+                out=hidden[:, t, :],
+                in_=bank[:],
+                func=ACT.Relu,
+                bias=bias1[:, column : column + 1],
+                scale=1.0,
+            )
+
+        w2_codes = [keep.tile([P, DIST], U32, name="w2_codes%d" % i, align_bytes=64) for i in (0, 1)]
+        w2_scales = [keep.tile([P, DIST], U8, name="w2_scales%d" % i, align_bytes=64) for i in (0, 1)]
+        bias2 = keep.tile([P, 2, DIST], F32)
+        result = keep.tile([P, 2, 2, ROWS, STOC], F32)
+        exp_neg = keep.tile([P, 2, ROWS, STOC], F32)
+        mean_rows = [o.rearrange("(p j) d -> p j d", j=ROWS) for o in (out_2, out_0)]
+        std_rows = [o.rearrange("(p j) d -> p j d", j=ROWS) for o in (out_3, out_1)]
+
+        def regroup(hidden):
+            grouped = stage.tile([P, GROUP, PACK], BF16, name="hidden_grouped", align_bytes=64)
+            nc.vector.tensor_copy(
+                out=grouped[:].rearrange("p (c i) t -> p c t i", i=4),
+                in_=hidden[:].rearrange("p t (c i) -> p c t i", i=4),
+            )
+            return grouped
+
+        def quantise_hidden(grouped):
+            codes = quantised.tile([P, GROUP], U32, name="hidden_codes", align_bytes=64)
+            scales = quantised.tile([P, GROUP], U8, name="hidden_scales", align_bytes=64)
+            nc.vector.quantize_mx(
+                out=codes[:].bitcast(FP8X4),
+                scales=scales[:],
+                in_=grouped[:].rearrange("p c t -> p (c t)"),
+            )
+            return codes, scales
+
+        def second_layer(step, codes, scales):
+            g, head = divmod(step, 2)
+            tiles = slice(g * TILES, (g + 1) * TILES)
+            bank = psum_second.tile([P, TILES, DIST], F32, name="head_bank")
+            for j in range(TILES):
+                rows = slice(j * P, (j + 1) * P)
+                nc.tensor.matmul_mx(
+                    out=bank[:, j, :],
+                    lhsT=codes[:, rows].bitcast(FP8X4),
+                    lhsT_scale=scales[:, rows],
+                    rhs=w2_codes[head][:].bitcast(FP8X4),
+                    rhs_scale=w2_scales[head][:],
+                    start=True,
+                    stop=True,
+                )
+            nc.vector.tensor_tensor(
+                out=result[:, head, :, tiles, :].rearrange("p f j d -> p j f d"),
+                in0=bank[:].rearrange("p j (f d) -> p j f d", f=2),
+                in1=bias2[:, head, :]
+                .rearrange("p (f d) -> p f d", f=2)
+                .unsqueeze(1)
+                .to_broadcast([P, TILES, 2, STOC]),
+                op=ALU.add,
+            )
+            nc.sync.dma_start(out=mean_rows[head][:, tiles, :], in_=result[:, head, 0, tiles, :])
+
+        def softplus_exp(step):
+            g, head = divmod(step, 2)
+            tiles = slice(g * TILES, (g + 1) * TILES)
+            magnitude = stage.tile([P, TILES, STOC], F32, name="magnitude")
+            nc.scalar.activation(out=magnitude[:], in_=result[:, head, 1, tiles, :], func=ACT.Abs)
+            nc.scalar.activation(
+                out=exp_neg[:, head, tiles, :], in_=magnitude[:], func=ACT.Exp, scale=-1.0
+            )
+
+        def softplus_linear(step):
+            g, head = divmod(step, 2)
+            v = result[:, head, 1, g * TILES : (g + 1) * TILES, :]
+            nc.vector.tensor_scalar(
+                out=v, in0=v, scalar1=0.0, scalar2=0.1, op0=ALU.max, op1=ALU.add
+            )
+
+        def softplus_log(g):
+            tiles = slice(g * TILES, (g + 1) * TILES)
+            for head in (PRIOR, POST):
+                log_term = exp_neg[:, head, tiles, :]
+                std = result[:, head, 1, tiles, :]
+                nc.scalar.activation(
+                    out=log_term, in_=log_term, func=ACT.Ln, bias=one_column[:], scale=1.0
+                )
+                nc.vector.tensor_tensor(out=std, in0=std, in1=log_term, op=ALU.add)
+                nc.sync.dma_start(out=std_rows[head][:, tiles, :], in_=std)
+
+        transpose_pass(0)
+        empty_bank(0, 0)
+        empty_bank(0, 1)
+        transpose_pass(1)
+        empty_bank(1, 0)
+        empty_bank(1, 1)
+        quantise_pass(0)
+        bias1_bank = psum_t.tile([P, P], BF16, name="bank")
+        nc.tensor.transpose(bias1_bank[:], bias1_rows[:], ident_bf16[:])
+        nc.vector.tensor_copy(out=bias1[:], in_=bias1_bank[:, 0 : 2 * CHUNKS])
+        quantise_pass(1)
+        hidden_banks = [first_layer_bank(0, t) for t in range(CHUNKS)]
+        for n in range(2, FIRST_IN_LOOP):
+            transpose_pass(n)
+            empty_bank(n, 0)
+            empty_bank(n, 1)
+            if n > 2:
+                quantise_pass(n - 1)
+        w2_grouped = []
+        for head in (PRIOR, POST):
+            w2_bank = psum_t.tile([P, CHUNKS, DIST], BF16, name="bank")
+            for t in range(CHUNKS):
+                nc.tensor.transpose(
+                    w2_bank[:, t, :], w2_raw[head][:, t * P : (t + 1) * P], ident_bf16[:]
+                )
+            grouped = keep.tile([P, DIST, PACK], BF16, name="w2_grouped%d" % head, align_bytes=64)
+            nc.vector.tensor_copy(out=grouped[:], in_=w2_bank[:].rearrange("p t d -> p d t"))
+            w2_grouped.append(grouped)
+        for head in (PRIOR, POST):
+            nc.vector.quantize_mx(
+                out=w2_codes[head][:].bitcast(FP8X4),
+                scales=w2_scales[head][:],
+                in_=w2_grouped[head][:].rearrange("p d t -> p (d t)"),
+            )
+        bias2_bank = psum_t.tile([P, 2 * DIST], F32, name="bank")
+        nc.tensor.matmul(out=bias2_bank[:], lhsT=ones[:], rhs=bias2_row[:], start=True, stop=True)
+        nc.vector.tensor_copy(out=bias2[:].rearrange("p h d -> p (h d)"), in_=bias2_bank[:])
+
+        hidden_of = {}
+        hidden_operand_of = {}
+        for s in range(STEPS + 3):
+            arriving = FIRST_IN_LOOP + s
+            if arriving - 1 < len(operand_passes):
+                quantise_pass(arriving - 1)
+            if 0 <= s - 2 < STEPS:
+                codes, scales = hidden_operand_of[s - 2]
+                second_layer(s - 2, codes, scales)
+            if 0 <= s - 1 < STEPS:
+                grouped = regroup(hidden_of[s - 1])
+            if arriving < len(operand_passes):
+                transpose_pass(arriving)
+                empty_bank(arriving, 1)
+            if 0 <= s - 1 < STEPS:
+                hidden_operand_of[s - 1] = quantise_hidden(grouped)
+            if s < STEPS:
+                hidden_of[s] = stage.tile([P, CHUNKS, GROUP], BF16, name="hidden")
+                next_banks = []
+                for t in range(CHUNKS):
+                    relu_out(s, t, hidden_banks[t], hidden_of[s])
+                    if s + 1 < STEPS:
+                        next_banks.append(first_layer_bank(s + 1, t))
+                hidden_banks = next_banks
+            if arriving < len(operand_passes):
+                empty_bank(arriving, 0)
+            if 0 <= s - 2 < STEPS:
+                softplus_exp(s - 2)
+            if 0 <= s - 3 < STEPS:
+                softplus_linear(s - 3)
+
+        for g in range(GROUPS):
+            softplus_log(g)

@@ -1,3 +1,4 @@
+import math
 from contextlib import ExitStack
 
 import concourse.mybir as mybir
@@ -29,6 +30,7 @@ GROUPS = ROWS // TILES
 
 PRIOR, POST = 0, 1
 STEPS = 2 * GROUPS
+SIGMOID_LAG = 6
 
 FLOPS = 2 * BATCH * (HID * K_PASS + HID * 2 * K_PASS + 2 * DIST * HID)
 
@@ -42,8 +44,7 @@ def tile_rssmcell_pb_t_kernel(
         raw = ctx.enter_context(tc.tile_pool(name="raw", bufs=GROUPS))
         stage = ctx.enter_context(tc.tile_pool(name="stage", bufs=3))
         quantised = ctx.enter_context(tc.tile_pool(name="quantised", bufs=4))
-        psum_t = ctx.enter_context(tc.psum_pool(name="psum_t", bufs=2))
-        psum_first = ctx.enter_context(tc.psum_pool(name="psum_first", bufs=5))
+        psum_ring = ctx.enter_context(tc.psum_pool(name="psum_ring", bufs=7))
         psum_second = ctx.enter_context(tc.psum_pool(name="psum_second", bufs=1))
         ctx.enter_context(tc.manual_schedule())
 
@@ -71,22 +72,28 @@ def tile_rssmcell_pb_t_kernel(
         wp1_raw = keep.tile([P, CHUNKS, K_PASS], BF16)
         nc.sync.dma_start(out=wp1_raw[:], in_=wp1.rearrange("(t p) k -> p t k", p=P))
         h_raw = [load_group(h_rows, 0, "h_raw")]
-        nc.sync.dma_start(out=bias1_rows[0:CHUNKS, :], in_=bp1.rearrange("(t p) -> t p", p=P))
-        nc.sync.dma_start(
+        nc.scalar.dma_start(out=bias1_rows[0:CHUNKS, :], in_=bp1.rearrange("(t p) -> t p", p=P))
+        nc.scalar.dma_start(
             out=bias1_rows[CHUNKS : 2 * CHUNKS, :], in_=bq1.rearrange("(t p) -> t p", p=P)
         )
-        wq1_raw = keep.tile([P, CHUNKS, 2 * K_PASS], BF16)
-        nc.sync.dma_start(out=wq1_raw[:], in_=wq1.rearrange("(t p) k -> p t k", p=P))
-        e_raw = [load_group(e_rows, 0, "e_raw")]
+        nc.scalar.dma_start(out=bias2_row[0:1, 0:DIST], in_=bp2.rearrange("(o d) -> o d", o=1))
+        nc.scalar.dma_start(
+            out=bias2_row[0:1, DIST : 2 * DIST], in_=bq2.rearrange("(o d) -> o d", o=1)
+        )
         w2_raw = []
         for head, w2 in ((PRIOR, wp2), (POST, wq2)):
             tile = keep.tile([P, HID], BF16, name="w2_raw%d" % head)
             nc.sync.dma_start(out=tile[:], in_=w2)
             w2_raw.append(tile)
-        nc.sync.dma_start(out=bias2_row[0:1, 0:DIST], in_=bp2.rearrange("(o d) -> o d", o=1))
-        nc.sync.dma_start(
-            out=bias2_row[0:1, DIST : 2 * DIST], in_=bq2.rearrange("(o d) -> o d", o=1)
-        )
+        table_warmer = keep.tile([P, 1], F32)
+        nc.scalar.activation(out=table_warmer[:], in_=one_column[:], func=ACT.Sigmoid)
+        wq1_raw = keep.tile([P, 2, CHUNKS, K_PASS], BF16)
+        for c in range(2):
+            nc.sync.dma_start(
+                out=wq1_raw[:, c, :, :],
+                in_=wq1[:, c * K_PASS : (c + 1) * K_PASS].rearrange("(t p) k -> p t k", p=P),
+            )
+        e_raw = [load_group(e_rows, 0, "e_raw")]
         for g in range(1, GROUPS):
             h_raw.append(load_group(h_rows, g, "h_raw"))
             e_raw.append(load_group(e_rows, g, "e_raw"))
@@ -103,8 +110,8 @@ def tile_rssmcell_pb_t_kernel(
         operand_passes = [
             (wp1_raw[:].bitcast(F32), w1_codes[PRIOR][:, 0, :], w1_scales[PRIOR][:, 0, :]),
             (h_raw[0][:].bitcast(F32), None, None),
-            (wq1_words[:, :, 0:WORDS], w1_codes[POST][:, 0, :], w1_scales[POST][:, 0, :]),
-            (wq1_words[:, :, WORDS : 2 * WORDS], w1_codes[POST][:, 1, :], w1_scales[POST][:, 1, :]),
+            (wq1_words[:, 0, :, :], w1_codes[POST][:, 0, :], w1_scales[POST][:, 0, :]),
+            (wq1_words[:, 1, :, :], w1_codes[POST][:, 1, :], w1_scales[POST][:, 1, :]),
             (e_raw[0][:].bitcast(F32), None, None),
         ]
         for g in range(1, GROUPS):
@@ -125,7 +132,7 @@ def tile_rssmcell_pb_t_kernel(
             words = operand_passes[n][0]
             banks = []
             for half in range(2):
-                bank = psum_t.tile([P, 2, 2 * P], F32, name="bank")
+                bank = psum_ring.tile([P, 2, 2 * P], F32, name="words_bank", tag="ring")
                 for r in range(2):
                     for u in range(2):
                         nc.tensor.transpose(
@@ -161,7 +168,7 @@ def tile_rssmcell_pb_t_kernel(
 
         def first_layer_bank(step, t):
             g, head = divmod(step, 2)
-            bank = psum_first.tile([P, GROUP], F32, name="hidden_bank")
+            bank = psum_ring.tile([P, GROUP], F32, name="hidden_bank", tag="ring")
             units = slice(t * P, (t + 1) * P)
             passes = 1 + head
             for c in range(passes):
@@ -191,7 +198,7 @@ def tile_rssmcell_pb_t_kernel(
         w2_scales = [keep.tile([P, DIST], U8, name="w2_scales%d" % i, align_bytes=64) for i in (0, 1)]
         bias2 = keep.tile([P, 2, DIST], F32)
         result = keep.tile([P, 2, 2, ROWS, STOC], F32)
-        exp_neg = keep.tile([P, 2, ROWS, STOC], F32)
+        sigmoid = keep.tile([P, 2, ROWS, STOC], F32)
         mean_rows = [o.rearrange("(p j) d -> p j d", j=ROWS) for o in (out_2, out_0)]
         std_rows = [o.rearrange("(p j) d -> p j d", j=ROWS) for o in (out_3, out_1)]
 
@@ -216,7 +223,7 @@ def tile_rssmcell_pb_t_kernel(
         def second_layer(step, codes, scales):
             g, head = divmod(step, 2)
             tiles = slice(g * TILES, (g + 1) * TILES)
-            bank = psum_second.tile([P, TILES, DIST], F32, name="head_bank")
+            bank = psum_second.tile([P, TILES, DIST], F32, name="head_bank", tag="second")
             for j in range(TILES):
                 rows = slice(j * P, (j + 1) * P)
                 nc.tensor.matmul_mx(
@@ -239,82 +246,87 @@ def tile_rssmcell_pb_t_kernel(
             )
             nc.sync.dma_start(out=mean_rows[head][:, tiles, :], in_=result[:, head, 0, tiles, :])
 
-        def softplus_exp(step):
+        def softplus_sigmoid(step):
             g, head = divmod(step, 2)
             tiles = slice(g * TILES, (g + 1) * TILES)
             magnitude = stage.tile([P, TILES, STOC], F32, name="magnitude")
             nc.scalar.activation(out=magnitude[:], in_=result[:, head, 1, tiles, :], func=ACT.Abs)
-            nc.scalar.activation(
-                out=exp_neg[:, head, tiles, :], in_=magnitude[:], func=ACT.Exp, scale=-1.0
-            )
-
-        def softplus_linear(step):
-            g, head = divmod(step, 2)
-            v = result[:, head, 1, g * TILES : (g + 1) * TILES, :]
-            nc.vector.tensor_scalar(
-                out=v, in0=v, scalar1=0.0, scalar2=0.1, op0=ALU.max, op1=ALU.add
-            )
+            nc.scalar.activation(out=sigmoid[:, head, tiles, :], in_=magnitude[:], func=ACT.Sigmoid)
 
         def softplus_log(g):
             tiles = slice(g * TILES, (g + 1) * TILES)
+            log_term = sigmoid[:, :, tiles, :]
+            std = result[:, :, 1, tiles, :]
+            nc.scalar.activation(out=log_term, in_=log_term, func=ACT.Ln, scale=math.exp(-0.1))
+            nc.vector.scalar_tensor_tensor(
+                out=std, in0=std, scalar=0.0, in1=log_term, op0=ALU.max, op1=ALU.subtract
+            )
             for head in (PRIOR, POST):
-                log_term = exp_neg[:, head, tiles, :]
-                std = result[:, head, 1, tiles, :]
-                nc.scalar.activation(
-                    out=log_term, in_=log_term, func=ACT.Ln, bias=one_column[:], scale=1.0
-                )
-                nc.vector.tensor_tensor(out=std, in0=std, in1=log_term, op=ALU.add)
-                nc.sync.dma_start(out=std_rows[head][:, tiles, :], in_=std)
+                nc.sync.dma_start(out=std_rows[head][:, tiles, :], in_=result[:, head, 1, tiles, :])
 
-        transpose_pass(0)
-        empty_bank(0, 0)
-        empty_bank(0, 1)
-        transpose_pass(1)
-        empty_bank(1, 0)
-        empty_bank(1, 1)
-        quantise_pass(0)
-        bias1_bank = psum_t.tile([P, P], BF16, name="bank")
-        nc.tensor.transpose(bias1_bank[:], bias1_rows[:], ident_bf16[:])
-        nc.vector.tensor_copy(out=bias1[:], in_=bias1_bank[:, 0 : 2 * CHUNKS])
-        quantise_pass(1)
-        hidden_banks = [first_layer_bank(0, t) for t in range(CHUNKS)]
-        for n in range(2, FIRST_IN_LOOP):
-            transpose_pass(n)
-            empty_bank(n, 0)
-            empty_bank(n, 1)
-            if n > 2:
-                quantise_pass(n - 1)
-        w2_grouped = []
-        for head in (PRIOR, POST):
-            w2_bank = psum_t.tile([P, CHUNKS, DIST], BF16, name="bank")
+        def transpose_bias1():
+            bank = psum_second.tile([P, P], BF16, name="bias1_bank", tag="second")
+            nc.tensor.transpose(bank[:], bias1_rows[:], ident_bf16[:])
+            nc.scalar.copy(out=bias1[:], in_=bank[:, 0 : 2 * CHUNKS])
+
+        def spread_bias2():
+            bank = psum_second.tile([P, 2 * DIST], F32, name="bias2_bank", tag="second")
+            nc.tensor.matmul(out=bank[:], lhsT=ones[:], rhs=bias2_row[:], start=True, stop=True)
+            nc.scalar.copy(out=bias2[:].rearrange("p h d -> p (h d)"), in_=bank[:])
+
+        w2_grouped = [
+            keep.tile([P, DIST, PACK], BF16, name="w2_grouped%d" % i, align_bytes=64) for i in (0, 1)
+        ]
+
+        def transpose_w2(head):
+            bank = psum_second.tile([P, CHUNKS, DIST], BF16, name="w2_bank", tag="second")
             for t in range(CHUNKS):
                 nc.tensor.transpose(
-                    w2_bank[:, t, :], w2_raw[head][:, t * P : (t + 1) * P], ident_bf16[:]
+                    bank[:, t, :], w2_raw[head][:, t * P : (t + 1) * P], ident_bf16[:]
                 )
-            grouped = keep.tile([P, DIST, PACK], BF16, name="w2_grouped%d" % head, align_bytes=64)
-            nc.vector.tensor_copy(out=grouped[:], in_=w2_bank[:].rearrange("p t d -> p d t"))
-            w2_grouped.append(grouped)
-        for head in (PRIOR, POST):
+            nc.scalar.copy(out=w2_grouped[head][:], in_=bank[:].rearrange("p t d -> p d t"))
+
+        def quantise_w2(head):
             nc.vector.quantize_mx(
                 out=w2_codes[head][:].bitcast(FP8X4),
                 scales=w2_scales[head][:],
                 in_=w2_grouped[head][:].rearrange("p d t -> p (d t)"),
             )
-        bias2_bank = psum_t.tile([P, 2 * DIST], F32, name="bank")
-        nc.tensor.matmul(out=bias2_bank[:], lhsT=ones[:], rhs=bias2_row[:], start=True, stop=True)
-        nc.vector.tensor_copy(out=bias2[:].rearrange("p h d -> p (h d)"), in_=bias2_bank[:])
+
+        def transpose_and_empty(n):
+            transpose_pass(n)
+            empty_bank(n, 0)
+            empty_bank(n, 1)
+
+        transpose_and_empty(0)
+        transpose_and_empty(1)
+        quantise_pass(0)
+        transpose_bias1()
+        quantise_pass(1)
+        transpose_w2(PRIOR)
+        transpose_and_empty(2)
+        spread_bias2()
+        transpose_and_empty(3)
+        quantise_pass(2)
+        transpose_w2(POST)
+        transpose_and_empty(4)
+        quantise_pass(3)
+        quantise_pass(4)
+        quantise_w2(PRIOR)
+        quantise_w2(POST)
+        hidden_banks = [first_layer_bank(0, t) for t in range(CHUNKS)]
 
         hidden_of = {}
         hidden_operand_of = {}
-        for s in range(STEPS + 3):
+        for s in range(STEPS + SIGMOID_LAG + 1):
             arriving = FIRST_IN_LOOP + s
-            if arriving - 1 < len(operand_passes):
+            if FIRST_IN_LOOP <= arriving - 1 < len(operand_passes):
                 quantise_pass(arriving - 1)
+            if 0 <= s - 1 < STEPS:
+                grouped = regroup(hidden_of[s - 1])
             if 0 <= s - 2 < STEPS:
                 codes, scales = hidden_operand_of[s - 2]
                 second_layer(s - 2, codes, scales)
-            if 0 <= s - 1 < STEPS:
-                grouped = regroup(hidden_of[s - 1])
             if arriving < len(operand_passes):
                 transpose_pass(arriving)
                 empty_bank(arriving, 1)
@@ -330,10 +342,8 @@ def tile_rssmcell_pb_t_kernel(
                 hidden_banks = next_banks
             if arriving < len(operand_passes):
                 empty_bank(arriving, 0)
-            if 0 <= s - 2 < STEPS:
-                softplus_exp(s - 2)
-            if 0 <= s - 3 < STEPS:
-                softplus_linear(s - 3)
+            if 0 <= s - SIGMOID_LAG < STEPS:
+                softplus_sigmoid(s - SIGMOID_LAG)
 
         for g in range(GROUPS):
             softplus_log(g)

@@ -15,7 +15,6 @@ ALU = mybir.AluOpType
 P = 128
 PACK = 4
 K_PASS = P * PACK
-WORDS = K_PASS // 2
 
 BATCH = 4096
 HID = 512
@@ -29,74 +28,50 @@ GROUP = TILES * P
 GROUPS = ROWS // TILES
 
 PRIOR, POST = 0, 1
-STEPS = 2 * GROUPS
-SIGMOID_LAG = 6
+PRIOR_AHEAD = 1
+SOFTPLUS_LAG = 6
+LOG_GROUPS = 1
+
+RING = 6
 
 FLOPS = 2 * BATCH * (HID * K_PASS + HID * 2 * K_PASS + 2 * DIST * HID)
+
+
+def step_order():
+    steps = [(g, PRIOR) for g in range(PRIOR_AHEAD)]
+    for g in range(GROUPS):
+        if g + PRIOR_AHEAD < GROUPS:
+            steps.append((g + PRIOR_AHEAD, PRIOR))
+        steps.append((g, POST))
+    return steps
 
 
 def tile_rssmcell_pb_t_kernel(
     tc, h, embedding, wp1, bp1, wp2, bp2, wq1, bq1, wq2, bq2, out_0, out_1, out_2, out_3
 ):
     nc = tc.nc
+    steps = step_order()
     with ExitStack() as ctx:
         keep = ctx.enter_context(tc.tile_pool(name="keep", bufs=1))
         raw = ctx.enter_context(tc.tile_pool(name="raw", bufs=GROUPS))
         stage = ctx.enter_context(tc.tile_pool(name="stage", bufs=3))
         quantised = ctx.enter_context(tc.tile_pool(name="quantised", bufs=4))
-        psum_ring = ctx.enter_context(tc.psum_pool(name="psum_ring", bufs=7))
-        psum_second = ctx.enter_context(tc.psum_pool(name="psum_second", bufs=1))
+        psum_ring = ctx.enter_context(tc.psum_pool(name="psum_ring", bufs=RING))
+        psum_second = ctx.enter_context(tc.psum_pool(name="psum_second", bufs=8 - RING))
         ctx.enter_context(tc.manual_schedule())
 
-        ident_f32 = keep.tile([P, P], F32)
-        make_identity(nc, ident_f32[:])
-        ident_bf16 = keep.tile([P, P], BF16)
-        make_identity(nc, ident_bf16[:])
-        ones = keep.tile([P, P], BF16)
-        nc.vector.memset(ones[:], 1.0)
-        one_column = keep.tile([P, 1], F32)
-        nc.vector.memset(one_column[:], 1.0)
         bias1_rows = keep.tile([P, P], BF16)
         nc.vector.memset(bias1_rows[:], 0.0)
         bias2_row = keep.tile([P, 2 * DIST], BF16)
         nc.vector.memset(bias2_row[:], 0.0)
-
-        h_rows = h.rearrange("(p j) k -> p j k", j=ROWS)
-        e_rows = embedding.rearrange("(p j) k -> p j k", j=ROWS)
-
-        def load_group(rows, g, name):
-            tile = raw.tile([P, TILES, K_PASS], BF16, name=name)
-            nc.sync.dma_start(out=tile[:], in_=rows[:, g * TILES : (g + 1) * TILES, :])
-            return tile
-
-        wp1_raw = keep.tile([P, CHUNKS, K_PASS], BF16)
-        nc.sync.dma_start(out=wp1_raw[:], in_=wp1.rearrange("(t p) k -> p t k", p=P))
-        h_raw = [load_group(h_rows, 0, "h_raw")]
-        nc.scalar.dma_start(out=bias1_rows[0:CHUNKS, :], in_=bp1.rearrange("(t p) -> t p", p=P))
-        nc.scalar.dma_start(
-            out=bias1_rows[CHUNKS : 2 * CHUNKS, :], in_=bq1.rearrange("(t p) -> t p", p=P)
-        )
-        nc.scalar.dma_start(out=bias2_row[0:1, 0:DIST], in_=bp2.rearrange("(o d) -> o d", o=1))
-        nc.scalar.dma_start(
-            out=bias2_row[0:1, DIST : 2 * DIST], in_=bq2.rearrange("(o d) -> o d", o=1)
-        )
-        w2_raw = []
-        for head, w2 in ((PRIOR, wp2), (POST, wq2)):
-            tile = keep.tile([P, HID], BF16, name="w2_raw%d" % head)
-            nc.sync.dma_start(out=tile[:], in_=w2)
-            w2_raw.append(tile)
-        table_warmer = keep.tile([P, 1], F32)
-        nc.scalar.activation(out=table_warmer[:], in_=one_column[:], func=ACT.Sigmoid)
-        wq1_raw = keep.tile([P, 2, CHUNKS, K_PASS], BF16)
-        for c in range(2):
-            nc.sync.dma_start(
-                out=wq1_raw[:, c, :, :],
-                in_=wq1[:, c * K_PASS : (c + 1) * K_PASS].rearrange("(t p) k -> p t k", p=P),
-            )
-        e_raw = [load_group(e_rows, 0, "e_raw")]
-        for g in range(1, GROUPS):
-            h_raw.append(load_group(h_rows, g, "h_raw"))
-            e_raw.append(load_group(e_rows, g, "e_raw"))
+        ones = keep.tile([P, P], BF16)
+        nc.vector.memset(ones[:], 1.0)
+        one_column = keep.tile([P, 1], F32)
+        nc.vector.memset(one_column[:], 1.0)
+        ident_f32 = keep.tile([P, P], F32)
+        make_identity(nc, ident_f32[:])
+        ident_bf16 = keep.tile([P, P], BF16)
+        make_identity(nc, ident_bf16[:])
 
         w1_codes = [
             keep.tile([P, 1, HID], U32, name="wp1_codes", align_bytes=64),
@@ -106,30 +81,66 @@ def tile_rssmcell_pb_t_kernel(
             keep.tile([P, 1, HID], U8, name="wp1_scales", align_bytes=64),
             keep.tile([P, 2, HID], U8, name="wq1_scales", align_bytes=64),
         ]
-        wq1_words = wq1_raw[:].bitcast(F32)
-        operand_passes = [
-            (wp1_raw[:].bitcast(F32), w1_codes[PRIOR][:, 0, :], w1_scales[PRIOR][:, 0, :]),
-            (h_raw[0][:].bitcast(F32), None, None),
-            (wq1_words[:, 0, :, :], w1_codes[POST][:, 0, :], w1_scales[POST][:, 0, :]),
-            (wq1_words[:, 1, :, :], w1_codes[POST][:, 1, :], w1_scales[POST][:, 1, :]),
-            (e_raw[0][:].bitcast(F32), None, None),
-        ]
-        for g in range(1, GROUPS):
-            operand_passes.append((h_raw[g][:].bitcast(F32), None, None))
-            operand_passes.append((e_raw[g][:].bitcast(F32), None, None))
-        FIRST_IN_LOOP = 5
+        pass_words = []
+        pass_weight = []
+        pass_name = []
+        pass_of = {}
+        new_passes = []
 
-        def pass_of(source, g):
-            if g == 0:
-                return 1 if source == 0 else 4
-            return FIRST_IN_LOOP + 2 * (g - 1) + source
+        def load_weight_pass(head, w1, c):
+            tile = keep.tile([P, CHUNKS, K_PASS], BF16, name="w1_raw%d%d" % (head, c))
+            nc.sync.dma_start(
+                out=tile[:],
+                in_=w1[:, c * K_PASS : (c + 1) * K_PASS].rearrange("(t p) k -> p t k", p=P),
+            )
+            pass_words.append(tile[:].bitcast(F32))
+            pass_weight.append((head, c))
+            pass_name.append(None)
+            return len(pass_words) - 1
+
+        def load_group_pass(source, rows, g, name):
+            tile = raw.tile([P, TILES, K_PASS], BF16, name=name + "_raw")
+            nc.sync.dma_start(out=tile[:], in_=rows[:, g * TILES : (g + 1) * TILES, :])
+            pass_words.append(tile[:].bitcast(F32))
+            pass_weight.append(None)
+            pass_name.append(name)
+            pass_of[(source, g)] = len(pass_words) - 1
+            return len(pass_words) - 1
+
+        nc.scalar.dma_start(out=bias1_rows[0:CHUNKS, :], in_=bp1.rearrange("(t p) -> t p", p=P))
+        nc.scalar.dma_start(
+            out=bias1_rows[CHUNKS : 2 * CHUNKS, :], in_=bq1.rearrange("(t p) -> t p", p=P)
+        )
+        nc.scalar.dma_start(out=bias2_row[0:1, 0:DIST], in_=bp2.rearrange("(o d) -> o d", o=1))
+        nc.scalar.dma_start(
+            out=bias2_row[0:1, DIST : 2 * DIST], in_=bq2.rearrange("(o d) -> o d", o=1)
+        )
+        table_warmer = keep.tile([P, 1], F32)
+        nc.scalar.activation(out=table_warmer[:], in_=one_column[:], func=ACT.Sigmoid)
+        h_rows = h.rearrange("(p j) k -> p j k", j=ROWS)
+        e_rows = embedding.rearrange("(p j) k -> p j k", j=ROWS)
+        w2_raw = [keep.tile([P, HID], BF16, name="w2_raw%d" % i) for i in (0, 1)]
+        for step, (g, head) in enumerate(steps):
+            new = []
+            if head == PRIOR:
+                if g == 0:
+                    new.append(load_weight_pass(PRIOR, wp1, 0))
+                new.append(load_group_pass(0, h_rows, g, "h"))
+            else:
+                if g == 0:
+                    new.append(load_weight_pass(POST, wq1, 0))
+                    new.append(load_weight_pass(POST, wq1, 1))
+                new.append(load_group_pass(1, e_rows, g, "e"))
+            new_passes.append(new)
+            if step == 1:
+                nc.sync.dma_start(out=w2_raw[PRIOR][:], in_=wp2)
+                nc.sync.dma_start(out=w2_raw[POST][:], in_=wq2)
 
         grouped_of = {}
         banks_of = {}
         operand_of = {}
 
         def transpose_pass(n):
-            words = operand_passes[n][0]
             banks = []
             for half in range(2):
                 bank = psum_ring.tile([P, 2, 2 * P], F32, name="words_bank", tag="ring")
@@ -137,7 +148,7 @@ def tile_rssmcell_pb_t_kernel(
                     for u in range(2):
                         nc.tensor.transpose(
                             bank[:, u, r * P : (r + 1) * P],
-                            words[:, 2 * half + r, u * P : (u + 1) * P],
+                            pass_words[n][:, 2 * half + r, u * P : (u + 1) * P],
                             ident_f32[:],
                         )
                 banks.append(bank)
@@ -153,10 +164,13 @@ def tile_rssmcell_pb_t_kernel(
                 nc.vector.tensor_copy(out=out, in_=in_)
 
         def quantise_pass(n):
-            codes, scales = operand_passes[n][1], operand_passes[n][2]
-            if codes is None:
-                codes = quantised.tile([P, GROUP], U32, name="c_codes", align_bytes=64)[:]
-                scales = quantised.tile([P, GROUP], U8, name="c_scales", align_bytes=64)[:]
+            if pass_weight[n] is None:
+                name = pass_name[n]
+                codes = quantised.tile([P, GROUP], U32, name=name + "_codes", align_bytes=64)[:]
+                scales = quantised.tile([P, GROUP], U8, name=name + "_scales", align_bytes=64)[:]
+            else:
+                head, c = pass_weight[n]
+                codes, scales = w1_codes[head][:, c, :], w1_scales[head][:, c, :]
             nc.vector.quantize_mx(
                 out=codes.bitcast(FP8X4),
                 scales=scales,
@@ -167,12 +181,12 @@ def tile_rssmcell_pb_t_kernel(
         bias1 = keep.tile([P, 2 * CHUNKS], F32)
 
         def first_layer_bank(step, t):
-            g, head = divmod(step, 2)
+            g, head = steps[step]
             bank = psum_ring.tile([P, GROUP], F32, name="hidden_bank", tag="ring")
             units = slice(t * P, (t + 1) * P)
             passes = 1 + head
             for c in range(passes):
-                codes, scales = operand_of[pass_of(c, g)]
+                codes, scales = operand_of[pass_of[(c, g)]]
                 nc.tensor.matmul_mx(
                     out=bank[:],
                     lhsT=w1_codes[head][:, c, units].bitcast(FP8X4),
@@ -185,7 +199,7 @@ def tile_rssmcell_pb_t_kernel(
             return bank
 
         def relu_out(step, t, bank, hidden):
-            column = CHUNKS * (step % 2) + t
+            column = CHUNKS * steps[step][1] + t
             nc.scalar.activation(
                 out=hidden[:, t, :],
                 in_=bank[:],
@@ -221,7 +235,7 @@ def tile_rssmcell_pb_t_kernel(
             return codes, scales
 
         def second_layer(step, codes, scales):
-            g, head = divmod(step, 2)
+            g, head = steps[step]
             tiles = slice(g * TILES, (g + 1) * TILES)
             bank = psum_second.tile([P, TILES, DIST], F32, name="head_bank", tag="second")
             for j in range(TILES):
@@ -246,15 +260,24 @@ def tile_rssmcell_pb_t_kernel(
             )
             nc.sync.dma_start(out=mean_rows[head][:, tiles, :], in_=result[:, head, 0, tiles, :])
 
-        def softplus_sigmoid(step):
-            g, head = divmod(step, 2)
-            tiles = slice(g * TILES, (g + 1) * TILES)
+        def softplus_abs(step):
+            g, head = steps[step]
             magnitude = stage.tile([P, TILES, STOC], F32, name="magnitude")
-            nc.scalar.activation(out=magnitude[:], in_=result[:, head, 1, tiles, :], func=ACT.Abs)
-            nc.scalar.activation(out=sigmoid[:, head, tiles, :], in_=magnitude[:], func=ACT.Sigmoid)
+            nc.scalar.activation(
+                out=magnitude[:], in_=result[:, head, 1, g * TILES : (g + 1) * TILES, :], func=ACT.Abs
+            )
+            return magnitude
 
-        def softplus_log(g):
-            tiles = slice(g * TILES, (g + 1) * TILES)
+        def softplus_sigmoid(step, magnitude):
+            g, head = steps[step]
+            nc.scalar.activation(
+                out=sigmoid[:, head, g * TILES : (g + 1) * TILES, :],
+                in_=magnitude[:],
+                func=ACT.Sigmoid,
+            )
+
+        def softplus_log(first_group):
+            tiles = slice(first_group * TILES, (first_group + LOG_GROUPS) * TILES)
             log_term = sigmoid[:, :, tiles, :]
             std = result[:, :, 1, tiles, :]
             nc.scalar.activation(out=log_term, in_=log_term, func=ACT.Ln, scale=math.exp(-0.1))
@@ -293,57 +316,55 @@ def tile_rssmcell_pb_t_kernel(
                 in_=w2_grouped[head][:].rearrange("p d t -> p (d t)"),
             )
 
-        def transpose_and_empty(n):
-            transpose_pass(n)
-            empty_bank(n, 0)
-            empty_bank(n, 1)
-
-        transpose_and_empty(0)
-        transpose_and_empty(1)
-        quantise_pass(0)
-        transpose_bias1()
-        quantise_pass(1)
+        for step in (0, 1):
+            for n in new_passes[step]:
+                transpose_pass(n)
+                empty_bank(n, 0)
+                empty_bank(n, 1)
+            if step == 0:
+                transpose_bias1()
+                for n in new_passes[0]:
+                    quantise_pass(n)
         transpose_w2(PRIOR)
-        transpose_and_empty(2)
-        spread_bias2()
-        transpose_and_empty(3)
-        quantise_pass(2)
         transpose_w2(POST)
-        transpose_and_empty(4)
-        quantise_pass(3)
-        quantise_pass(4)
+        spread_bias2()
+        hidden_banks = [first_layer_bank(0, t) for t in range(CHUNKS)]
         quantise_w2(PRIOR)
         quantise_w2(POST)
-        hidden_banks = [first_layer_bank(0, t) for t in range(CHUNKS)]
 
+        n_steps = len(steps)
         hidden_of = {}
         hidden_operand_of = {}
-        for s in range(STEPS + SIGMOID_LAG + 1):
-            arriving = FIRST_IN_LOOP + s
-            if FIRST_IN_LOOP <= arriving - 1 < len(operand_passes):
-                quantise_pass(arriving - 1)
-            if 0 <= s - 1 < STEPS:
+        magnitude_of = {}
+        for s in range(n_steps + SOFTPLUS_LAG + 2):
+            arriving = new_passes[s + 2] if s + 2 < n_steps else []
+            if s + 1 < n_steps:
+                for n in new_passes[s + 1]:
+                    quantise_pass(n)
+            if 0 <= s - 1 < n_steps:
                 grouped = regroup(hidden_of[s - 1])
-            if 0 <= s - 2 < STEPS:
+            for n in arriving:
+                transpose_pass(n)
+                empty_bank(n, 1)
+            if 0 <= s - 1 < n_steps:
+                hidden_operand_of[s - 1] = quantise_hidden(grouped)
+            if 0 <= s - 2 < n_steps:
                 codes, scales = hidden_operand_of[s - 2]
                 second_layer(s - 2, codes, scales)
-            if arriving < len(operand_passes):
-                transpose_pass(arriving)
-                empty_bank(arriving, 1)
-            if 0 <= s - 1 < STEPS:
-                hidden_operand_of[s - 1] = quantise_hidden(grouped)
-            if s < STEPS:
+            if s < n_steps:
                 hidden_of[s] = stage.tile([P, CHUNKS, GROUP], BF16, name="hidden")
                 next_banks = []
                 for t in range(CHUNKS):
                     relu_out(s, t, hidden_banks[t], hidden_of[s])
-                    if s + 1 < STEPS:
+                    if s + 1 < n_steps:
                         next_banks.append(first_layer_bank(s + 1, t))
                 hidden_banks = next_banks
-            if arriving < len(operand_passes):
-                empty_bank(arriving, 0)
-            if 0 <= s - SIGMOID_LAG < STEPS:
-                softplus_sigmoid(s - SIGMOID_LAG)
+            for n in arriving:
+                empty_bank(n, 0)
+            if 0 <= s - SOFTPLUS_LAG < n_steps:
+                magnitude_of[s - SOFTPLUS_LAG] = softplus_abs(s - SOFTPLUS_LAG)
+            if 0 <= s - SOFTPLUS_LAG - 1 < n_steps:
+                softplus_sigmoid(s - SOFTPLUS_LAG - 1, magnitude_of[s - SOFTPLUS_LAG - 1])
 
-        for g in range(GROUPS):
-            softplus_log(g)
+        for first_group in range(0, GROUPS, LOG_GROUPS):
+            softplus_log(first_group)

@@ -155,10 +155,13 @@ def tile_rssmcell_pb_t_kernel(
             banks_of[n] = banks
             grouped_of[n] = stage.tile([P, GROUP, PACK], BF16, name="grouped", align_bytes=64)
 
+        def scalar_empties(n, half):
+            return half == 0 or n % 4 == 0
+
         def empty_bank(n, half):
             out = grouped_of[n][:].bitcast(F32)[:, half * 2 * P : (half + 1) * 2 * P, :]
             in_ = banks_of[n][half][:].rearrange("p u c -> p c u")
-            if half == 0:
+            if scalar_empties(n, half):
                 nc.scalar.copy(out=out, in_=in_)
             else:
                 nc.vector.tensor_copy(out=out, in_=in_)
@@ -345,7 +348,8 @@ def tile_rssmcell_pb_t_kernel(
                 grouped = regroup(hidden_of[s - 1])
             for n in arriving:
                 transpose_pass(n)
-                empty_bank(n, 1)
+                if not scalar_empties(n, 1):
+                    empty_bank(n, 1)
             if 0 <= s - 1 < n_steps:
                 hidden_operand_of[s - 1] = quantise_hidden(grouped)
             if 0 <= s - 2 < n_steps:
@@ -361,6 +365,8 @@ def tile_rssmcell_pb_t_kernel(
                 hidden_banks = next_banks
             for n in arriving:
                 empty_bank(n, 0)
+                if scalar_empties(n, 1):
+                    empty_bank(n, 1)
             if 0 <= s - SOFTPLUS_LAG < n_steps:
                 magnitude_of[s - SOFTPLUS_LAG] = softplus_abs(s - SOFTPLUS_LAG)
             if 0 <= s - SOFTPLUS_LAG - 1 < n_steps:

@@ -31,6 +31,7 @@ PRIOR, POST = 0, 1
 PRIOR_AHEAD = 1
 SOFTPLUS_LAG = 6
 LOG_GROUPS = 1
+LOG_CAP = 40.0
 
 RING = 6
 
@@ -116,7 +117,7 @@ def tile_rssmcell_pb_t_kernel(
             out=bias2_row[0:1, DIST : 2 * DIST], in_=bq2.rearrange("(o d) -> o d", o=1)
         )
         table_warmer = keep.tile([P, 1], F32)
-        nc.scalar.activation(out=table_warmer[:], in_=one_column[:], func=ACT.Sigmoid)
+        nc.scalar.activation(out=table_warmer[:], in_=one_column[:], func=ACT.Exp)
         h_rows = h.rearrange("(p j) k -> p j k", j=ROWS)
         e_rows = embedding.rearrange("(p j) k -> p j k", j=ROWS)
         w2_raw = [keep.tile([P, HID], BF16, name="w2_raw%d" % i) for i in (0, 1)]
@@ -156,7 +157,7 @@ def tile_rssmcell_pb_t_kernel(
             grouped_of[n] = stage.tile([P, GROUP, PACK], BF16, name="grouped", align_bytes=64)
 
         def scalar_empties(n, half):
-            return half == 0 or n % 4 == 0
+            return half == 0 or n % 2 == 0
 
         def empty_bank(n, half):
             out = grouped_of[n][:].bitcast(F32)[:, half * 2 * P : (half + 1) * 2 * P, :]
@@ -215,7 +216,7 @@ def tile_rssmcell_pb_t_kernel(
         w2_scales = [keep.tile([P, DIST], U8, name="w2_scales%d" % i, align_bytes=64) for i in (0, 1)]
         bias2 = keep.tile([P, 2, DIST], F32)
         result = keep.tile([P, 2, 2, ROWS, STOC], F32)
-        sigmoid = keep.tile([P, 2, ROWS, STOC], F32)
+        power = keep.tile([P, 2, ROWS, STOC], F32)
         mean_rows = [o.rearrange("(p j) d -> p j d", j=ROWS) for o in (out_2, out_0)]
         std_rows = [o.rearrange("(p j) d -> p j d", j=ROWS) for o in (out_3, out_1)]
 
@@ -263,29 +264,20 @@ def tile_rssmcell_pb_t_kernel(
             )
             nc.sync.dma_start(out=mean_rows[head][:, tiles, :], in_=result[:, head, 0, tiles, :])
 
-        def softplus_abs(step):
+        def softplus_exp(step):
             g, head = steps[step]
-            magnitude = stage.tile([P, TILES, STOC], F32, name="magnitude")
+            tiles = slice(g * TILES, (g + 1) * TILES)
             nc.scalar.activation(
-                out=magnitude[:], in_=result[:, head, 1, g * TILES : (g + 1) * TILES, :], func=ACT.Abs
-            )
-            return magnitude
-
-        def softplus_sigmoid(step, magnitude):
-            g, head = steps[step]
-            nc.scalar.activation(
-                out=sigmoid[:, head, g * TILES : (g + 1) * TILES, :],
-                in_=magnitude[:],
-                func=ACT.Sigmoid,
+                out=power[:, head, tiles, :], in_=result[:, head, 1, tiles, :], func=ACT.Exp
             )
 
         def softplus_log(first_group):
             tiles = slice(first_group * TILES, (first_group + LOG_GROUPS) * TILES)
-            log_term = sigmoid[:, :, tiles, :]
+            log_term = power[:, :, tiles, :]
             std = result[:, :, 1, tiles, :]
-            nc.scalar.activation(out=log_term, in_=log_term, func=ACT.Ln, scale=math.exp(-0.1))
+            nc.scalar.activation(out=log_term, in_=log_term, func=ACT.Ln, bias=math.exp(0.1))
             nc.vector.scalar_tensor_tensor(
-                out=std, in0=std, scalar=0.0, in1=log_term, op0=ALU.max, op1=ALU.subtract
+                out=std, in0=log_term, scalar=LOG_CAP, in1=std, op0=ALU.min, op1=ALU.max
             )
             for head in (PRIOR, POST):
                 nc.sync.dma_start(out=std_rows[head][:, tiles, :], in_=result[:, head, 1, tiles, :])
@@ -298,7 +290,12 @@ def tile_rssmcell_pb_t_kernel(
         def spread_bias2():
             bank = psum_second.tile([P, 2 * DIST], F32, name="bias2_bank", tag="second")
             nc.tensor.matmul(out=bank[:], lhsT=ones[:], rhs=bias2_row[:], start=True, stop=True)
-            nc.scalar.copy(out=bias2[:].rearrange("p h d -> p (h d)"), in_=bank[:])
+            for f in range(2):
+                nc.vector.tensor_scalar_add(
+                    out=bias2[:, :, f * STOC : (f + 1) * STOC],
+                    in0=bank[:].rearrange("p (h f d) -> p h f d", h=2, f=2)[:, :, f, :],
+                    scalar1=0.1 * f,
+                )
 
         w2_grouped = [
             keep.tile([P, DIST, PACK], BF16, name="w2_grouped%d" % i, align_bytes=64) for i in (0, 1)
@@ -338,8 +335,7 @@ def tile_rssmcell_pb_t_kernel(
         n_steps = len(steps)
         hidden_of = {}
         hidden_operand_of = {}
-        magnitude_of = {}
-        for s in range(n_steps + SOFTPLUS_LAG + 2):
+        for s in range(n_steps + SOFTPLUS_LAG):
             arriving = new_passes[s + 2] if s + 2 < n_steps else []
             if s + 1 < n_steps:
                 for n in new_passes[s + 1]:
@@ -368,9 +364,7 @@ def tile_rssmcell_pb_t_kernel(
                 if scalar_empties(n, 1):
                     empty_bank(n, 1)
             if 0 <= s - SOFTPLUS_LAG < n_steps:
-                magnitude_of[s - SOFTPLUS_LAG] = softplus_abs(s - SOFTPLUS_LAG)
-            if 0 <= s - SOFTPLUS_LAG - 1 < n_steps:
-                softplus_sigmoid(s - SOFTPLUS_LAG - 1, magnitude_of[s - SOFTPLUS_LAG - 1])
+                softplus_exp(s - SOFTPLUS_LAG)
 
         for first_group in range(0, GROUPS, LOG_GROUPS):
             softplus_log(first_group)

@@ -28,7 +28,7 @@ GROUP = TILES * P
 GROUPS = ROWS // TILES
 
 PRIOR, POST = 0, 1
-PRIOR_AHEAD = 1
+PRIOR_AHEAD = 2
 SOFTPLUS_LAG = 6
 LOG_GROUPS = 1
 LOG_CAP = 40.0
@@ -56,7 +56,7 @@ def tile_rssmcell_pb_t_kernel(
         keep = ctx.enter_context(tc.tile_pool(name="keep", bufs=1))
         raw = ctx.enter_context(tc.tile_pool(name="raw", bufs=GROUPS))
         stage = ctx.enter_context(tc.tile_pool(name="stage", bufs=3))
-        quantised = ctx.enter_context(tc.tile_pool(name="quantised", bufs=4))
+        quantised = ctx.enter_context(tc.tile_pool(name="quantised", bufs=6))
         psum_ring = ctx.enter_context(tc.psum_pool(name="psum_ring", bufs=RING))
         psum_second = ctx.enter_context(tc.psum_pool(name="psum_second", bufs=8 - RING))
         ctx.enter_context(tc.manual_schedule())
@@ -86,13 +86,15 @@ def tile_rssmcell_pb_t_kernel(
         pass_weight = []
         pass_name = []
         pass_of = {}
-        new_passes = []
+
+        def load_halves(tile, in_):
+            for rows in (slice(0, TILES // 2), slice(TILES // 2, TILES)):
+                nc.sync.dma_start(out=tile[:, rows, :], in_=in_[:, rows, :])
 
         def load_weight_pass(head, w1, c):
             tile = keep.tile([P, CHUNKS, K_PASS], BF16, name="w1_raw%d%d" % (head, c))
-            nc.sync.dma_start(
-                out=tile[:],
-                in_=w1[:, c * K_PASS : (c + 1) * K_PASS].rearrange("(t p) k -> p t k", p=P),
+            load_halves(
+                tile, w1[:, c * K_PASS : (c + 1) * K_PASS].rearrange("(t p) k -> p t k", p=P)
             )
             pass_words.append(tile[:].bitcast(F32))
             pass_weight.append((head, c))
@@ -101,7 +103,7 @@ def tile_rssmcell_pb_t_kernel(
 
         def load_group_pass(source, rows, g, name):
             tile = raw.tile([P, TILES, K_PASS], BF16, name=name + "_raw")
-            nc.sync.dma_start(out=tile[:], in_=rows[:, g * TILES : (g + 1) * TILES, :])
+            load_halves(tile, rows[:, g * TILES : (g + 1) * TILES, :])
             pass_words.append(tile[:].bitcast(F32))
             pass_weight.append(None)
             pass_name.append(name)
@@ -121,19 +123,17 @@ def tile_rssmcell_pb_t_kernel(
         h_rows = h.rearrange("(p j) k -> p j k", j=ROWS)
         e_rows = embedding.rearrange("(p j) k -> p j k", j=ROWS)
         w2_raw = [keep.tile([P, HID], BF16, name="w2_raw%d" % i) for i in (0, 1)]
+        arriving = {}
         for step, (g, head) in enumerate(steps):
-            new = []
-            if head == PRIOR:
-                if g == 0:
-                    new.append(load_weight_pass(PRIOR, wp1, 0))
-                new.append(load_group_pass(0, h_rows, g, "h"))
-            else:
-                if g == 0:
-                    new.append(load_weight_pass(POST, wq1, 0))
-                    new.append(load_weight_pass(POST, wq1, 1))
-                new.append(load_group_pass(1, e_rows, g, "e"))
-            new_passes.append(new)
-            if step == 1:
+            new = arriving.setdefault(step - 2, [])
+            if step == 0:
+                new.append(load_weight_pass(PRIOR, wp1, 0))
+            if head == POST and g == 0:
+                new.append(load_weight_pass(POST, wq1, 1))
+            new.append(load_group_pass(head, (h_rows, e_rows)[head], g, "he"[head]))
+            if step == PRIOR_AHEAD:
+                new.append(load_weight_pass(POST, wq1, 0))
+            if step == PRIOR_AHEAD + 1:
                 nc.sync.dma_start(out=w2_raw[PRIOR][:], in_=wp2)
                 nc.sync.dma_start(out=w2_raw[POST][:], in_=wq2)
 
@@ -202,11 +202,11 @@ def tile_rssmcell_pb_t_kernel(
                 )
             return bank
 
-        def relu_out(step, t, bank, hidden):
+        def relu_out(step, t, bank, hidden, cols):
             column = CHUNKS * steps[step][1] + t
             nc.scalar.activation(
-                out=hidden[:, t, :],
-                in_=bank[:],
+                out=hidden[:, t, cols],
+                in_=bank[:, cols],
                 func=ACT.Relu,
                 bias=bias1[:, column : column + 1],
                 scale=1.0,
@@ -220,30 +220,33 @@ def tile_rssmcell_pb_t_kernel(
         mean_rows = [o.rearrange("(p j) d -> p j d", j=ROWS) for o in (out_2, out_0)]
         std_rows = [o.rearrange("(p j) d -> p j d", j=ROWS) for o in (out_3, out_1)]
 
-        def regroup(hidden):
-            grouped = stage.tile([P, GROUP, PACK], BF16, name="hidden_grouped", align_bytes=64)
+        def regroup(hidden, grouped, cols):
             nc.vector.tensor_copy(
-                out=grouped[:].rearrange("p (c i) t -> p c t i", i=4),
-                in_=hidden[:].rearrange("p t (c i) -> p c t i", i=4),
+                out=grouped[:, cols, :].rearrange("p (c i) t -> p c t i", i=4),
+                in_=hidden[:, :, cols].rearrange("p t (c i) -> p c t i", i=4),
             )
-            return grouped
 
-        def quantise_hidden(grouped):
+        def hidden_tiles():
+            grouped = stage.tile([P, GROUP, PACK], BF16, name="hidden_grouped", align_bytes=64)
             codes = quantised.tile([P, GROUP], U32, name="hidden_codes", align_bytes=64)
             scales = quantised.tile([P, GROUP], U8, name="hidden_scales", align_bytes=64)
-            nc.vector.quantize_mx(
-                out=codes[:].bitcast(FP8X4),
-                scales=scales[:],
-                in_=grouped[:].rearrange("p c t -> p (c t)"),
-            )
-            return codes, scales
+            return grouped, codes, scales
 
-        def second_layer(step, codes, scales):
+        def quantise_hidden(grouped, codes, scales, cols):
+            nc.vector.quantize_mx(
+                out=codes[:, cols].bitcast(FP8X4),
+                scales=scales[:, cols],
+                in_=grouped[:, cols, :].rearrange("p c t -> p (c t)"),
+            )
+
+        def second_layer(step, codes, scales, cols):
             g, head = steps[step]
-            tiles = slice(g * TILES, (g + 1) * TILES)
-            bank = psum_second.tile([P, TILES, DIST], F32, name="head_bank", tag="second")
-            for j in range(TILES):
-                rows = slice(j * P, (j + 1) * P)
+            n_tiles = (cols.stop - cols.start) // P
+            first_tile = g * TILES + cols.start // P
+            tiles = slice(first_tile, first_tile + n_tiles)
+            bank = psum_second.tile([P, n_tiles, DIST], F32, name="head_bank", tag="second")
+            for j in range(n_tiles):
+                rows = slice(cols.start + j * P, cols.start + (j + 1) * P)
                 nc.tensor.matmul_mx(
                     out=bank[:, j, :],
                     lhsT=codes[:, rows].bitcast(FP8X4),
@@ -259,7 +262,7 @@ def tile_rssmcell_pb_t_kernel(
                 in1=bias2[:, head, :]
                 .rearrange("p (f d) -> p f d", f=2)
                 .unsqueeze(1)
-                .to_broadcast([P, TILES, 2, STOC]),
+                .to_broadcast([P, n_tiles, 2, STOC]),
                 op=ALU.add,
             )
             nc.sync.dma_start(out=mean_rows[head][:, tiles, :], in_=result[:, head, 0, tiles, :])
@@ -316,55 +319,76 @@ def tile_rssmcell_pb_t_kernel(
                 in_=w2_grouped[head][:].rearrange("p d t -> p (d t)"),
             )
 
-        for step in (0, 1):
-            for n in new_passes[step]:
-                transpose_pass(n)
-                empty_bank(n, 0)
-                empty_bank(n, 1)
-            if step == 0:
-                transpose_bias1()
-                for n in new_passes[0]:
-                    quantise_pass(n)
-        transpose_w2(PRIOR)
-        transpose_w2(POST)
+        for n in arriving[-2]:
+            transpose_pass(n)
+            empty_bank(n, 0)
+            empty_bank(n, 1)
+        transpose_bias1()
         spread_bias2()
+        for n in arriving[-1]:
+            transpose_pass(n)
+            empty_bank(n, 0)
+        for n in arriving[-2]:
+            quantise_pass(n)
+        for n in arriving[-1]:
+            empty_bank(n, 1)
         hidden_banks = [first_layer_bank(0, t) for t in range(CHUNKS)]
-        quantise_w2(PRIOR)
-        quantise_w2(POST)
 
         n_steps = len(steps)
+        whole = slice(0, GROUP)
+        halves = [slice(0, GROUP // 2), slice(GROUP // 2, GROUP)]
         hidden_of = {}
-        hidden_operand_of = {}
-        for s in range(n_steps + SOFTPLUS_LAG):
-            arriving = new_passes[s + 2] if s + 2 < n_steps else []
-            if s + 1 < n_steps:
-                for n in new_passes[s + 1]:
-                    quantise_pass(n)
-            if 0 <= s - 1 < n_steps:
-                grouped = regroup(hidden_of[s - 1])
-            for n in arriving:
+        tiles_of = {}
+        for s in range(n_steps):
+            here = arriving.get(s, [])
+            for n in arriving.get(s - 1, []):
+                quantise_pass(n)
+            if s == 2:
+                quantise_w2(PRIOR)
+                quantise_w2(POST)
+            if s >= 1:
+                tiles_of[s - 1] = hidden_tiles()
+                regroup(hidden_of[s - 1], tiles_of[s - 1][0], whole)
+            for n in here:
                 transpose_pass(n)
+            if s >= 2:
+                second_layer(s - 2, *tiles_of[s - 2][1:], whole)
+            for n in here:
                 if not scalar_empties(n, 1):
                     empty_bank(n, 1)
-            if 0 <= s - 1 < n_steps:
-                hidden_operand_of[s - 1] = quantise_hidden(grouped)
-            if 0 <= s - 2 < n_steps:
-                codes, scales = hidden_operand_of[s - 2]
-                second_layer(s - 2, codes, scales)
-            if s < n_steps:
-                hidden_of[s] = stage.tile([P, CHUNKS, GROUP], BF16, name="hidden")
+            if s >= 1:
+                quantise_hidden(*tiles_of[s - 1], whole)
+            hidden_of[s] = stage.tile([P, CHUNKS, GROUP], BF16, name="hidden")
+            if s + 1 < n_steps:
                 next_banks = []
                 for t in range(CHUNKS):
-                    relu_out(s, t, hidden_banks[t], hidden_of[s])
-                    if s + 1 < n_steps:
-                        next_banks.append(first_layer_bank(s + 1, t))
+                    relu_out(s, t, hidden_banks[t], hidden_of[s], whole)
+                    next_banks.append(first_layer_bank(s + 1, t))
                 hidden_banks = next_banks
-            for n in arriving:
+            else:
+                for cols in halves:
+                    for t in range(CHUNKS):
+                        relu_out(s, t, hidden_banks[t], hidden_of[s], cols)
+            for n in here:
                 empty_bank(n, 0)
                 if scalar_empties(n, 1):
                     empty_bank(n, 1)
-            if 0 <= s - SOFTPLUS_LAG < n_steps:
+            if s == 1:
+                transpose_w2(PRIOR)
+                transpose_w2(POST)
+            if s >= SOFTPLUS_LAG:
                 softplus_exp(s - SOFTPLUS_LAG)
 
+        last = n_steps - 1
+        tiles_of[last] = hidden_tiles()
+        regroup(hidden_of[last], tiles_of[last][0], halves[0])
+        second_layer(last - 1, *tiles_of[last - 1][1:], whole)
+        quantise_hidden(*tiles_of[last], halves[0])
+        regroup(hidden_of[last], tiles_of[last][0], halves[1])
+        second_layer(last, *tiles_of[last][1:], halves[0])
+        quantise_hidden(*tiles_of[last], halves[1])
+        second_layer(last, *tiles_of[last][1:], halves[1])
+        for s in range(n_steps - SOFTPLUS_LAG, n_steps):
+            softplus_exp(s)
         for first_group in range(0, GROUPS, LOG_GROUPS):
             softplus_log(first_group)

@@ -61,8 +61,6 @@ def tile_rssmcell_pb_t_kernel(
         psum_second = ctx.enter_context(tc.psum_pool(name="psum_second", bufs=8 - RING))
         ctx.enter_context(tc.manual_schedule())
 
-        bias1_rows = keep.tile([P, P], BF16)
-        nc.vector.memset(bias1_rows[:], 0.0)
         bias2_row = keep.tile([P, 2 * DIST], BF16)
         nc.vector.memset(bias2_row[:], 0.0)
         ones = keep.tile([P, P], BF16)
@@ -87,14 +85,11 @@ def tile_rssmcell_pb_t_kernel(
         pass_name = []
         pass_of = {}
 
-        def load_halves(tile, in_):
-            for rows in (slice(0, TILES // 2), slice(TILES // 2, TILES)):
-                nc.sync.dma_start(out=tile[:, rows, :], in_=in_[:, rows, :])
-
         def load_weight_pass(head, w1, c):
             tile = keep.tile([P, CHUNKS, K_PASS], BF16, name="w1_raw%d%d" % (head, c))
-            load_halves(
-                tile, w1[:, c * K_PASS : (c + 1) * K_PASS].rearrange("(t p) k -> p t k", p=P)
+            nc.sync.dma_start(
+                out=tile[:],
+                in_=w1[:, c * K_PASS : (c + 1) * K_PASS].rearrange("(p t) k -> p t k", p=P),
             )
             pass_words.append(tile[:].bitcast(F32))
             pass_weight.append((head, c))
@@ -103,17 +98,16 @@ def tile_rssmcell_pb_t_kernel(
 
         def load_group_pass(source, rows, g, name):
             tile = raw.tile([P, TILES, K_PASS], BF16, name=name + "_raw")
-            load_halves(tile, rows[:, g * TILES : (g + 1) * TILES, :])
+            nc.sync.dma_start(out=tile[:], in_=rows[:, g * TILES : (g + 1) * TILES, :])
             pass_words.append(tile[:].bitcast(F32))
             pass_weight.append(None)
             pass_name.append(name)
             pass_of[(source, g)] = len(pass_words) - 1
             return len(pass_words) - 1
 
-        nc.scalar.dma_start(out=bias1_rows[0:CHUNKS, :], in_=bp1.rearrange("(t p) -> t p", p=P))
-        nc.scalar.dma_start(
-            out=bias1_rows[CHUNKS : 2 * CHUNKS, :], in_=bq1.rearrange("(t p) -> t p", p=P)
-        )
+        bias1 = [keep.tile([P, CHUNKS], BF16, name="bias1_%d" % i) for i in (0, 1)]
+        nc.scalar.dma_start(out=bias1[PRIOR][:], in_=bp1.rearrange("(p t) -> p t", p=P))
+        nc.scalar.dma_start(out=bias1[POST][:], in_=bq1.rearrange("(p t) -> p t", p=P))
         nc.scalar.dma_start(out=bias2_row[0:1, 0:DIST], in_=bp2.rearrange("(o d) -> o d", o=1))
         nc.scalar.dma_start(
             out=bias2_row[0:1, DIST : 2 * DIST], in_=bq2.rearrange("(o d) -> o d", o=1)
@@ -182,8 +176,6 @@ def tile_rssmcell_pb_t_kernel(
             )
             operand_of[n] = (codes, scales)
 
-        bias1 = keep.tile([P, 2 * CHUNKS], F32)
-
         def first_layer_bank(step, t):
             g, head = steps[step]
             bank = psum_ring.tile([P, GROUP], F32, name="hidden_bank", tag="ring")
@@ -203,12 +195,12 @@ def tile_rssmcell_pb_t_kernel(
             return bank
 
         def relu_out(step, t, bank, hidden, cols):
-            column = CHUNKS * steps[step][1] + t
+            head = steps[step][1]
             nc.scalar.activation(
                 out=hidden[:, t, cols],
                 in_=bank[:, cols],
                 func=ACT.Relu,
-                bias=bias1[:, column : column + 1],
+                bias=bias1[head][:, t : t + 1],
                 scale=1.0,
             )
 
@@ -285,11 +277,6 @@ def tile_rssmcell_pb_t_kernel(
             for head in (PRIOR, POST):
                 nc.sync.dma_start(out=std_rows[head][:, tiles, :], in_=result[:, head, 1, tiles, :])
 
-        def transpose_bias1():
-            bank = psum_second.tile([P, P], BF16, name="bias1_bank", tag="second")
-            nc.tensor.transpose(bank[:], bias1_rows[:], ident_bf16[:])
-            nc.scalar.copy(out=bias1[:], in_=bank[:, 0 : 2 * CHUNKS])
-
         def spread_bias2():
             bank = psum_second.tile([P, 2 * DIST], F32, name="bias2_bank", tag="second")
             nc.tensor.matmul(out=bank[:], lhsT=ones[:], rhs=bias2_row[:], start=True, stop=True)
@@ -308,7 +295,7 @@ def tile_rssmcell_pb_t_kernel(
             bank = psum_second.tile([P, CHUNKS, DIST], BF16, name="w2_bank", tag="second")
             for t in range(CHUNKS):
                 nc.tensor.transpose(
-                    bank[:, t, :], w2_raw[head][:, t * P : (t + 1) * P], ident_bf16[:]
+                    bank[:, t, :], w2_raw[head][:, t:HID:CHUNKS], ident_bf16[:]
                 )
             nc.scalar.copy(out=w2_grouped[head][:], in_=bank[:].rearrange("p t d -> p d t"))
 
@@ -323,7 +310,6 @@ def tile_rssmcell_pb_t_kernel(
             transpose_pass(n)
             empty_bank(n, 0)
             empty_bank(n, 1)
-        transpose_bias1()
         spread_bias2()
         for n in arriving[-1]:
             transpose_pass(n)

@@ -85,16 +85,17 @@ def tile_rssmcell_pb_t_kernel(
         pass_name = []
         pass_of = {}
 
-        def load_weight_pass(head, w1, c):
-            tile = keep.tile([P, CHUNKS, K_PASS], BF16, name="w1_raw%d%d" % (head, c))
-            nc.sync.dma_start(
-                out=tile[:],
-                in_=w1[:, c * K_PASS : (c + 1) * K_PASS].rearrange("(p t) k -> p t k", p=P),
-            )
-            pass_words.append(tile[:].bitcast(F32))
-            pass_weight.append((head, c))
-            pass_name.append(None)
-            return len(pass_words) - 1
+        def load_weight(head, w1, pieces):
+            tile = keep.tile([P, CHUNKS, (1 + head) * K_PASS], BF16, name="w1_raw%d" % head)
+            rows = w1.rearrange("(p t) k -> p t k", p=P)
+            for t in range(0, CHUNKS, CHUNKS // pieces):
+                piece = slice(t, t + CHUNKS // pieces)
+                nc.sync.dma_start(out=tile[:, piece, :], in_=rows[:, piece, :])
+            for c in range(1 + head):
+                pass_words.append(tile[:, :, c * K_PASS : (c + 1) * K_PASS].bitcast(F32))
+                pass_weight.append((head, c))
+                pass_name.append(None)
+            return list(range(len(pass_words) - 1 - head, len(pass_words)))
 
         def load_group_pass(source, rows, g, name):
             tile = raw.tile([P, TILES, K_PASS], BF16, name=name + "_raw")
@@ -117,52 +118,59 @@ def tile_rssmcell_pb_t_kernel(
         h_rows = h.rearrange("(p j) k -> p j k", j=ROWS)
         e_rows = embedding.rearrange("(p j) k -> p j k", j=ROWS)
         w2_raw = [keep.tile([P, HID], BF16, name="w2_raw%d" % i) for i in (0, 1)]
-        arriving = {}
-        for step, (g, head) in enumerate(steps):
-            new = arriving.setdefault(step - 2, [])
-            if step == 0:
-                new.append(load_weight_pass(PRIOR, wp1, 0))
-            if head == POST and g == 0:
-                new.append(load_weight_pass(POST, wq1, 1))
-            new.append(load_group_pass(head, (h_rows, e_rows)[head], g, "he"[head]))
-            if step == PRIOR_AHEAD:
-                new.append(load_weight_pass(POST, wq1, 0))
-            if step == PRIOR_AHEAD + 1:
-                nc.sync.dma_start(out=w2_raw[PRIOR][:], in_=wp2)
-                nc.sync.dma_start(out=w2_raw[POST][:], in_=wq2)
+        h_pass = {}
+        e_pass = {}
+        h_pass[0] = load_group_pass(0, h_rows, 0, "h")
+        [wp1_pass] = load_weight(PRIOR, wp1, 2)
+        h_pass[1] = load_group_pass(0, h_rows, 1, "h")
+        h_pass[2] = load_group_pass(0, h_rows, 2, "h")
+        wq1_pass = load_weight(POST, wq1, 1)
+        e_pass[0] = load_group_pass(1, e_rows, 0, "e")
+        nc.sync.dma_start(out=w2_raw[PRIOR][:], in_=wp2)
+        nc.sync.dma_start(out=w2_raw[POST][:], in_=wq2)
+        for g in range(1, GROUPS):
+            if g + PRIOR_AHEAD < GROUPS:
+                h_pass[g + PRIOR_AHEAD] = load_group_pass(0, h_rows, g + PRIOR_AHEAD, "h")
+            e_pass[g] = load_group_pass(1, e_rows, g, "e")
+        arriving = {step - 2: [(h_pass, e_pass)[head][g]] for step, (g, head) in enumerate(steps)}
+        arriving[0].append(wq1_pass[0])
+        arriving[1].append(wq1_pass[1])
 
         grouped_of = {}
         banks_of = {}
         operand_of = {}
 
+        def transpose_half(n, half):
+            bank = psum_ring.tile([P, 2, 2 * P], F32, name="words_bank", tag="ring")
+            for r in range(2):
+                for u in range(2):
+                    nc.tensor.transpose(
+                        bank[:, u, r * P : (r + 1) * P],
+                        pass_words[n][:, 2 * half + r, u * P : (u + 1) * P],
+                        ident_f32[:],
+                    )
+            banks_of[n, half] = bank
+
         def transpose_pass(n):
-            banks = []
-            for half in range(2):
-                bank = psum_ring.tile([P, 2, 2 * P], F32, name="words_bank", tag="ring")
-                for r in range(2):
-                    for u in range(2):
-                        nc.tensor.transpose(
-                            bank[:, u, r * P : (r + 1) * P],
-                            pass_words[n][:, 2 * half + r, u * P : (u + 1) * P],
-                            ident_f32[:],
-                        )
-                banks.append(bank)
-            banks_of[n] = banks
             grouped_of[n] = stage.tile([P, GROUP, PACK], BF16, name="grouped", align_bytes=64)
+            transpose_half(n, 0)
+            transpose_half(n, 1)
 
         def scalar_empties(n, half):
             return half == 0 or n % 2 == 0
 
-        def empty_bank(n, half):
+        def empty_bank(n, half, by_scalar):
             out = grouped_of[n][:].bitcast(F32)[:, half * 2 * P : (half + 1) * 2 * P, :]
-            in_ = banks_of[n][half][:].rearrange("p u c -> p c u")
-            if scalar_empties(n, half):
+            in_ = banks_of[n, half][:].rearrange("p u c -> p c u")
+            if by_scalar:
                 nc.scalar.copy(out=out, in_=in_)
             else:
                 nc.vector.tensor_copy(out=out, in_=in_)
 
-        def quantise_pass(n):
-            if pass_weight[n] is None:
+        def quantise_pass(n, cols):
+            if n in operand_of:
+                codes, scales = operand_of[n]
+            elif pass_weight[n] is None:
                 name = pass_name[n]
                 codes = quantised.tile([P, GROUP], U32, name=name + "_codes", align_bytes=64)[:]
                 scales = quantised.tile([P, GROUP], U8, name=name + "_scales", align_bytes=64)[:]
@@ -170,9 +178,9 @@ def tile_rssmcell_pb_t_kernel(
                 head, c = pass_weight[n]
                 codes, scales = w1_codes[head][:, c, :], w1_scales[head][:, c, :]
             nc.vector.quantize_mx(
-                out=codes.bitcast(FP8X4),
-                scales=scales,
-                in_=grouped_of[n][:].rearrange("p c t -> p (c t)"),
+                out=codes[:, cols].bitcast(FP8X4),
+                scales=scales[:, cols],
+                in_=grouped_of[n][:, cols, :].rearrange("p c t -> p (c t)"),
             )
             operand_of[n] = (codes, scales)
 
@@ -306,29 +314,31 @@ def tile_rssmcell_pb_t_kernel(
                 in_=w2_grouped[head][:].rearrange("p d t -> p (d t)"),
             )
 
-        for n in arriving[-2]:
-            transpose_pass(n)
-            empty_bank(n, 0)
-            empty_bank(n, 1)
+        whole = slice(0, GROUP)
+        halves = [slice(0, GROUP // 2), slice(GROUP // 2, GROUP)]
+        h0, h1 = h_pass[0], h_pass[1]
+        transpose_pass(h0)
+        empty_bank(h0, 0, True)
+        empty_bank(h0, 1, False)
+        transpose_pass(wp1_pass)
+        quantise_pass(h0, whole)
+        empty_bank(wp1_pass, 0, True)
+        empty_bank(wp1_pass, 1, True)
         spread_bias2()
-        for n in arriving[-1]:
-            transpose_pass(n)
-            empty_bank(n, 0)
-        for n in arriving[-2]:
-            quantise_pass(n)
-        for n in arriving[-1]:
-            empty_bank(n, 1)
+        quantise_pass(wp1_pass, halves[0])
+        quantise_pass(wp1_pass, halves[1])
+        transpose_pass(h1)
+        empty_bank(h1, 0, True)
+        empty_bank(h1, 1, False)
         hidden_banks = [first_layer_bank(0, t) for t in range(CHUNKS)]
 
         n_steps = len(steps)
-        whole = slice(0, GROUP)
-        halves = [slice(0, GROUP // 2), slice(GROUP // 2, GROUP)]
         hidden_of = {}
         tiles_of = {}
         for s in range(n_steps):
             here = arriving.get(s, [])
             for n in arriving.get(s - 1, []):
-                quantise_pass(n)
+                quantise_pass(n, whole)
             if s == 2:
                 quantise_w2(PRIOR)
                 quantise_w2(POST)
@@ -341,7 +351,7 @@ def tile_rssmcell_pb_t_kernel(
                 second_layer(s - 2, *tiles_of[s - 2][1:], whole)
             for n in here:
                 if not scalar_empties(n, 1):
-                    empty_bank(n, 1)
+                    empty_bank(n, 1, False)
             if s >= 1:
                 quantise_hidden(*tiles_of[s - 1], whole)
             hidden_of[s] = stage.tile([P, CHUNKS, GROUP], BF16, name="hidden")
@@ -356,9 +366,9 @@ def tile_rssmcell_pb_t_kernel(
                     for t in range(CHUNKS):
                         relu_out(s, t, hidden_banks[t], hidden_of[s], cols)
             for n in here:
-                empty_bank(n, 0)
+                empty_bank(n, 0, True)
                 if scalar_empties(n, 1):
-                    empty_bank(n, 1)
+                    empty_bank(n, 1, True)
             if s == 1:
                 transpose_w2(PRIOR)
                 transpose_w2(POST)

@@ -97,9 +97,12 @@ def tile_rssmcell_pb_t_kernel(
                 pass_name.append(None)
             return list(range(len(pass_words) - 1 - head, len(pass_words)))
 
-        def load_group_pass(source, rows, g, name):
+        def load_group_pass(source, rows, g, name, pieces=1):
             tile = raw.tile([P, TILES, K_PASS], BF16, name=name + "_raw")
-            nc.sync.dma_start(out=tile[:], in_=rows[:, g * TILES : (g + 1) * TILES, :])
+            for j in range(0, TILES, TILES // pieces):
+                piece = slice(j, j + TILES // pieces)
+                rows_in = slice(g * TILES + j, g * TILES + j + TILES // pieces)
+                nc.sync.dma_start(out=tile[:, piece, :], in_=rows[:, rows_in, :])
             pass_words.append(tile[:].bitcast(F32))
             pass_weight.append(None)
             pass_name.append(name)
@@ -120,7 +123,7 @@ def tile_rssmcell_pb_t_kernel(
         w2_raw = [keep.tile([P, HID], BF16, name="w2_raw%d" % i) for i in (0, 1)]
         h_pass = {}
         e_pass = {}
-        h_pass[0] = load_group_pass(0, h_rows, 0, "h")
+        h_pass[0] = load_group_pass(0, h_rows, 0, "h", 2)
         [wp1_pass] = load_weight(PRIOR, wp1, 2)
         h_pass[1] = load_group_pass(0, h_rows, 1, "h")
         h_pass[2] = load_group_pass(0, h_rows, 2, "h")
@@ -157,7 +160,7 @@ def tile_rssmcell_pb_t_kernel(
             transpose_half(n, 1)
 
         def scalar_empties(n, half):
-            return half == 0 or n % 2 == 0
+            return half == 0 or (n >= 6 and n % 2 == 0)
 
         def empty_bank(n, half, by_scalar):
             out = grouped_of[n][:].bitcast(F32)[:, half * 2 * P : (half + 1) * 2 * P, :]
@@ -226,6 +229,12 @@ def tile_rssmcell_pb_t_kernel(
                 in_=hidden[:, :, cols].rearrange("p t (c i) -> p c t i", i=4),
             )
 
+        def regroup_scalar(hidden, grouped, cols):
+            nc.scalar.copy(
+                out=grouped[:, cols, :].rearrange("p (c i) t -> p c t i", i=4),
+                in_=hidden[:, :, cols].rearrange("p t (c i) -> p c t i", i=4),
+            )
+
         def hidden_tiles():
             grouped = stage.tile([P, GROUP, PACK], BF16, name="hidden_grouped", align_bytes=64)
             codes = quantised.tile([P, GROUP], U32, name="hidden_codes", align_bytes=64)
@@ -267,11 +276,10 @@ def tile_rssmcell_pb_t_kernel(
             )
             nc.sync.dma_start(out=mean_rows[head][:, tiles, :], in_=result[:, head, 0, tiles, :])
 
-        def softplus_exp(step):
-            g, head = steps[step]
+        def softplus_exp(g, heads=slice(0, 2)):
             tiles = slice(g * TILES, (g + 1) * TILES)
             nc.scalar.activation(
-                out=power[:, head, tiles, :], in_=result[:, head, 1, tiles, :], func=ACT.Exp
+                out=power[:, heads, tiles, :], in_=result[:, heads, 1, tiles, :], func=ACT.Exp
             )
 
         def softplus_log(first_group):
@@ -321,19 +329,22 @@ def tile_rssmcell_pb_t_kernel(
         empty_bank(h0, 0, True)
         empty_bank(h0, 1, False)
         transpose_pass(wp1_pass)
-        quantise_pass(h0, whole)
         empty_bank(wp1_pass, 0, True)
+        quantise_pass(h0, whole)
         empty_bank(wp1_pass, 1, True)
-        spread_bias2()
         quantise_pass(wp1_pass, halves[0])
         quantise_pass(wp1_pass, halves[1])
+        hidden_banks = [first_layer_bank(0, t) for t in (0, 1)]
         transpose_pass(h1)
-        empty_bank(h1, 0, True)
+        hidden_banks += [first_layer_bank(0, t) for t in (2, 3)]
         empty_bank(h1, 1, False)
-        hidden_banks = [first_layer_bank(0, t) for t in range(CHUNKS)]
+        hidden_of = {0: stage.tile([P, CHUNKS, GROUP], BF16, name="hidden")}
+        relu_out(0, 0, hidden_banks[0], hidden_of[0], whole)
+        relu_out(0, 1, hidden_banks[1], hidden_of[0], whole)
+        empty_bank(h1, 0, True)
+        spread_bias2()
 
         n_steps = len(steps)
-        hidden_of = {}
         tiles_of = {}
         for s in range(n_steps):
             here = arriving.get(s, [])
@@ -354,11 +365,13 @@ def tile_rssmcell_pb_t_kernel(
                     empty_bank(n, 1, False)
             if s >= 1:
                 quantise_hidden(*tiles_of[s - 1], whole)
-            hidden_of[s] = stage.tile([P, CHUNKS, GROUP], BF16, name="hidden")
+            if s > 0:
+                hidden_of[s] = stage.tile([P, CHUNKS, GROUP], BF16, name="hidden")
             if s + 1 < n_steps:
                 next_banks = []
                 for t in range(CHUNKS):
-                    relu_out(s, t, hidden_banks[t], hidden_of[s], whole)
+                    if s > 0 or t > 1:
+                        relu_out(s, t, hidden_banks[t], hidden_of[s], whole)
                     next_banks.append(first_layer_bank(s + 1, t))
                 hidden_banks = next_banks
             else:
@@ -372,19 +385,22 @@ def tile_rssmcell_pb_t_kernel(
             if s == 1:
                 transpose_w2(PRIOR)
                 transpose_w2(POST)
-            if s >= SOFTPLUS_LAG:
-                softplus_exp(s - SOFTPLUS_LAG)
+            if s >= SOFTPLUS_LAG and steps[s - SOFTPLUS_LAG][1] == POST:
+                softplus_exp(steps[s - SOFTPLUS_LAG][0])
 
         last = n_steps - 1
         tiles_of[last] = hidden_tiles()
         regroup(hidden_of[last], tiles_of[last][0], halves[0])
         second_layer(last - 1, *tiles_of[last - 1][1:], whole)
         quantise_hidden(*tiles_of[last], halves[0])
-        regroup(hidden_of[last], tiles_of[last][0], halves[1])
+        regroup_scalar(hidden_of[last], tiles_of[last][0], halves[1])
         second_layer(last, *tiles_of[last][1:], halves[0])
         quantise_hidden(*tiles_of[last], halves[1])
         second_layer(last, *tiles_of[last][1:], halves[1])
-        for s in range(n_steps - SOFTPLUS_LAG, n_steps):
-            softplus_exp(s)
+        for g in range(GROUPS):
+            if g < GROUPS - 1 and steps.index((g, POST)) + SOFTPLUS_LAG >= n_steps:
+                softplus_exp(g)
+        softplus_exp(GROUPS - 1, slice(PRIOR, PRIOR + 1))
+        softplus_exp(GROUPS - 1, slice(POST, POST + 1))
         for first_group in range(0, GROUPS, LOG_GROUPS):
             softplus_log(first_group)

@@ -30,7 +30,6 @@ GROUPS = ROWS // TILES
 PRIOR, POST = 0, 1
 PRIOR_AHEAD = 2
 SOFTPLUS_LAG = 6
-LOG_GROUPS = 1
 LOG_CAP = 40.0
 
 RING = 6
@@ -110,12 +109,6 @@ def tile_rssmcell_pb_t_kernel(
             return len(pass_words) - 1
 
         bias1 = [keep.tile([P, CHUNKS], BF16, name="bias1_%d" % i) for i in (0, 1)]
-        nc.scalar.dma_start(out=bias1[PRIOR][:], in_=bp1.rearrange("(p t) -> p t", p=P))
-        nc.scalar.dma_start(out=bias1[POST][:], in_=bq1.rearrange("(p t) -> p t", p=P))
-        nc.scalar.dma_start(out=bias2_row[0:1, 0:DIST], in_=bp2.rearrange("(o d) -> o d", o=1))
-        nc.scalar.dma_start(
-            out=bias2_row[0:1, DIST : 2 * DIST], in_=bq2.rearrange("(o d) -> o d", o=1)
-        )
         table_warmer = keep.tile([P, 1], F32)
         nc.scalar.activation(out=table_warmer[:], in_=one_column[:], func=ACT.Exp)
         h_rows = h.rearrange("(p j) k -> p j k", j=ROWS)
@@ -125,6 +118,12 @@ def tile_rssmcell_pb_t_kernel(
         e_pass = {}
         h_pass[0] = load_group_pass(0, h_rows, 0, "h", 2)
         [wp1_pass] = load_weight(PRIOR, wp1, 2)
+        nc.sync.dma_start(out=bias1[PRIOR][:], in_=bp1.rearrange("(p t) -> p t", p=P))
+        nc.sync.dma_start(out=bias1[POST][:], in_=bq1.rearrange("(p t) -> p t", p=P))
+        nc.sync.dma_start(out=bias2_row[0:1, 0:DIST], in_=bp2.rearrange("(o d) -> o d", o=1))
+        nc.sync.dma_start(
+            out=bias2_row[0:1, DIST : 2 * DIST], in_=bq2.rearrange("(o d) -> o d", o=1)
+        )
         h_pass[1] = load_group_pass(0, h_rows, 1, "h")
         h_pass[2] = load_group_pass(0, h_rows, 2, "h")
         wq1_pass = load_weight(POST, wq1, 1)
@@ -282,16 +281,14 @@ def tile_rssmcell_pb_t_kernel(
                 out=power[:, heads, tiles, :], in_=result[:, heads, 1, tiles, :], func=ACT.Exp
             )
 
-        def softplus_log(first_group):
-            tiles = slice(first_group * TILES, (first_group + LOG_GROUPS) * TILES)
-            log_term = power[:, :, tiles, :]
-            std = result[:, :, 1, tiles, :]
+        def softplus_log(head, tiles):
+            log_term = power[:, head, tiles, :]
+            std = result[:, head, 1, tiles, :]
             nc.scalar.activation(out=log_term, in_=log_term, func=ACT.Ln, bias=math.exp(0.1))
             nc.vector.scalar_tensor_tensor(
                 out=std, in0=log_term, scalar=LOG_CAP, in1=std, op0=ALU.min, op1=ALU.max
             )
-            for head in (PRIOR, POST):
-                nc.sync.dma_start(out=std_rows[head][:, tiles, :], in_=result[:, head, 1, tiles, :])
+            nc.sync.dma_start(out=std_rows[head][:, tiles, :], in_=std)
 
         def spread_bias2():
             bank = psum_second.tile([P, 2 * DIST], F32, name="bias2_bank", tag="second")
@@ -402,5 +399,8 @@ def tile_rssmcell_pb_t_kernel(
                 softplus_exp(g)
         softplus_exp(GROUPS - 1, slice(PRIOR, PRIOR + 1))
         softplus_exp(GROUPS - 1, slice(POST, POST + 1))
-        for first_group in range(0, GROUPS, LOG_GROUPS):
-            softplus_log(first_group)
+        for head, pieces in ((PRIOR, (4, 8, 8, 12)), (POST, (12, 8, 8, 4))):
+            first = 0
+            for n_tiles in pieces:
+                softplus_log(head, slice(first, first + n_tiles))
+                first += n_tiles

@@ -224,8 +224,8 @@ def tile_rssmcell_pb_t_kernel(
 
         def regroup(hidden, grouped, cols):
             nc.vector.tensor_copy(
-                out=grouped[:, cols, :].rearrange("p (c i) t -> p c t i", i=4),
-                in_=hidden[:, :, cols].rearrange("p t (c i) -> p c t i", i=4),
+                out=grouped[:, cols, :].rearrange("p (c i) t -> p c t i", i=8),
+                in_=hidden[:, :, cols].rearrange("p t (c i) -> p c t i", i=8),
             )
 
         def regroup_scalar(hidden, grouped, cols):

@@ -126,8 +126,8 @@ def tile_rssmcell_pb_t_kernel(
         )
         h_pass[1] = load_group_pass(0, h_rows, 1, "h")
         h_pass[2] = load_group_pass(0, h_rows, 2, "h")
-        wq1_pass = load_weight(POST, wq1, 1)
         e_pass[0] = load_group_pass(1, e_rows, 0, "e")
+        wq1_pass = load_weight(POST, wq1, 1)
         nc.sync.dma_start(out=w2_raw[PRIOR][:], in_=wp2)
         nc.sync.dma_start(out=w2_raw[POST][:], in_=wq2)
         for g in range(1, GROUPS):
@@ -135,8 +135,8 @@ def tile_rssmcell_pb_t_kernel(
                 h_pass[g + PRIOR_AHEAD] = load_group_pass(0, h_rows, g + PRIOR_AHEAD, "h")
             e_pass[g] = load_group_pass(1, e_rows, g, "e")
         arriving = {step - 2: [(h_pass, e_pass)[head][g]] for step, (g, head) in enumerate(steps)}
-        arriving[0].append(wq1_pass[0])
-        arriving[1].append(wq1_pass[1])
+        arriving[0].append(e_pass[0])
+        arriving[1] = wq1_pass
 
         grouped_of = {}
         banks_of = {}

@@ -29,6 +29,7 @@ GROUPS = ROWS // TILES
 
 PRIOR, POST = 0, 1
 PRIOR_AHEAD = 2
+G_COLS = 128
 SOFTPLUS_LAG = 6
 LOG_CAP = 40.0
 
@@ -119,7 +120,6 @@ def tile_rssmcell_pb_t_kernel(
         h_pass[0] = load_group_pass(0, h_rows, 0, "h", 2)
         [wp1_pass] = load_weight(PRIOR, wp1, 2)
         nc.sync.dma_start(out=bias1[PRIOR][:], in_=bp1.rearrange("(p t) -> p t", p=P))
-        nc.sync.dma_start(out=bias1[POST][:], in_=bq1.rearrange("(p t) -> p t", p=P))
         nc.sync.dma_start(out=bias2_row[0:1, 0:DIST], in_=bp2.rearrange("(o d) -> o d", o=1))
         nc.sync.dma_start(
             out=bias2_row[0:1, DIST : 2 * DIST], in_=bq2.rearrange("(o d) -> o d", o=1)
@@ -128,6 +128,7 @@ def tile_rssmcell_pb_t_kernel(
         h_pass[2] = load_group_pass(0, h_rows, 2, "h")
         e_pass[0] = load_group_pass(1, e_rows, 0, "e")
         wq1_pass = load_weight(POST, wq1, 1)
+        nc.sync.dma_start(out=bias1[POST][:], in_=bq1.rearrange("(p t) -> p t", p=P))
         nc.sync.dma_start(out=w2_raw[PRIOR][:], in_=wp2)
         nc.sync.dma_start(out=w2_raw[POST][:], in_=wq2)
         for g in range(1, GROUPS):
@@ -159,7 +160,7 @@ def tile_rssmcell_pb_t_kernel(
             transpose_half(n, 1)
 
         def scalar_empties(n, half):
-            return half == 0 or (n >= 6 and n % 2 == 0)
+            return half == 0 or (n >= 6 and n % 4 == 2)
 
         def empty_bank(n, half, by_scalar):
             out = grouped_of[n][:].bitcast(F32)[:, half * 2 * P : (half + 1) * 2 * P, :]
@@ -226,6 +227,16 @@ def tile_rssmcell_pb_t_kernel(
             nc.vector.tensor_copy(
                 out=grouped[:, cols, :].rearrange("p (c i) t -> p c t i", i=8),
                 in_=hidden[:, :, cols].rearrange("p t (c i) -> p c t i", i=8),
+            )
+
+        def regroup_gpsimd(hidden, grouped, cols):
+            nc.gpsimd.tensor_scalar(
+                out=grouped[:, cols, :].rearrange("p (c i) t -> p c t i", i=8),
+                in0=hidden[:, :, cols].rearrange("p t (c i) -> p c t i", i=8),
+                scalar1=1.0,
+                scalar2=0.0,
+                op0=ALU.mult,
+                op1=ALU.add,
             )
 
         def regroup_scalar(hidden, grouped, cols):
@@ -352,7 +363,10 @@ def tile_rssmcell_pb_t_kernel(
                 quantise_w2(POST)
             if s >= 1:
                 tiles_of[s - 1] = hidden_tiles()
-                regroup(hidden_of[s - 1], tiles_of[s - 1][0], whole)
+                g_cols = G_COLS if s > 2 else 0
+                if g_cols:
+                    regroup_gpsimd(hidden_of[s - 1], tiles_of[s - 1][0], slice(0, g_cols))
+                regroup(hidden_of[s - 1], tiles_of[s - 1][0], slice(g_cols, GROUP))
             for n in here:
                 transpose_pass(n)
             if s >= 2:

import math
from contextlib import ExitStack

import concourse.mybir as mybir
from concourse.masks import make_identity

F32 = mybir.dt.float32
BF16 = mybir.dt.bfloat16
U32 = mybir.dt.uint32
U8 = mybir.dt.uint8
FP8X4 = mybir.dt.float8_e4m3fn_x4
ACT = mybir.ActivationFunctionType
ALU = mybir.AluOpType

P = 128
PACK = 4
K_PASS = P * PACK

BATCH = 4096
HID = 512
DIST = 128
STOC = DIST // 2
CHUNKS = HID // P

ROWS = BATCH // P
TILES = 4
GROUP = TILES * P
GROUPS = ROWS // TILES

PRIOR, POST = 0, 1
PRIOR_AHEAD = 2
G_COLS = 128
SOFTPLUS_LAG = 6
LOG_CAP = 40.0

RING = 6

FLOPS = 2 * BATCH * (HID * K_PASS + HID * 2 * K_PASS + 2 * DIST * HID)


def step_order():
    steps = [(g, PRIOR) for g in range(PRIOR_AHEAD)]
    for g in range(GROUPS):
        if g + PRIOR_AHEAD < GROUPS:
            steps.append((g + PRIOR_AHEAD, PRIOR))
        steps.append((g, POST))
    return steps


def tile_rssmcell_pb_t_kernel(
    tc, h, embedding, wp1, bp1, wp2, bp2, wq1, bq1, wq2, bq2, out_0, out_1, out_2, out_3
):
    nc = tc.nc
    steps = step_order()
    with ExitStack() as ctx:
        keep = ctx.enter_context(tc.tile_pool(name="keep", bufs=1))
        raw = ctx.enter_context(tc.tile_pool(name="raw", bufs=GROUPS))
        stage = ctx.enter_context(tc.tile_pool(name="stage", bufs=3))
        quantised = ctx.enter_context(tc.tile_pool(name="quantised", bufs=6))
        psum_ring = ctx.enter_context(tc.psum_pool(name="psum_ring", bufs=RING))
        psum_second = ctx.enter_context(tc.psum_pool(name="psum_second", bufs=8 - RING))
        ctx.enter_context(tc.manual_schedule())

        bias2_row = keep.tile([P, 2 * DIST], BF16)
        nc.vector.memset(bias2_row[:], 0.0)
        ones = keep.tile([P, P], BF16)
        nc.vector.memset(ones[:], 1.0)
        one_column = keep.tile([P, 1], F32)
        nc.vector.memset(one_column[:], 1.0)
        ident_f32 = keep.tile([P, P], F32)
        make_identity(nc, ident_f32[:])
        ident_bf16 = keep.tile([P, P], BF16)
        make_identity(nc, ident_bf16[:])

        w1_codes = [
            keep.tile([P, 1, HID], U32, name="wp1_codes", align_bytes=64),
            keep.tile([P, 2, HID], U32, name="wq1_codes", align_bytes=64),
        ]
        w1_scales = [
            keep.tile([P, 1, HID], U8, name="wp1_scales", align_bytes=64),
            keep.tile([P, 2, HID], U8, name="wq1_scales", align_bytes=64),
        ]
        pass_words = []
        pass_weight = []
        pass_name = []
        pass_of = {}

        def load_weight(head, w1, pieces):
            tile = keep.tile([P, CHUNKS, (1 + head) * K_PASS], BF16, name="w1_raw%d" % head)
            rows = w1.rearrange("(p t) k -> p t k", p=P)
            for t in range(0, CHUNKS, CHUNKS // pieces):
                piece = slice(t, t + CHUNKS // pieces)
                nc.sync.dma_start(out=tile[:, piece, :], in_=rows[:, piece, :])
            for c in range(1 + head):
                pass_words.append(tile[:, :, c * K_PASS : (c + 1) * K_PASS].bitcast(F32))
                pass_weight.append((head, c))
                pass_name.append(None)
            return list(range(len(pass_words) - 1 - head, len(pass_words)))

        def load_group_pass(source, rows, g, name, pieces=1):
            tile = raw.tile([P, TILES, K_PASS], BF16, name=name + "_raw")
            for j in range(0, TILES, TILES // pieces):
                piece = slice(j, j + TILES // pieces)
                rows_in = slice(g * TILES + j, g * TILES + j + TILES // pieces)
                nc.sync.dma_start(out=tile[:, piece, :], in_=rows[:, rows_in, :])
            pass_words.append(tile[:].bitcast(F32))
            pass_weight.append(None)
            pass_name.append(name)
            pass_of[(source, g)] = len(pass_words) - 1
            return len(pass_words) - 1

        bias1 = [keep.tile([P, CHUNKS], BF16, name="bias1_%d" % i) for i in (0, 1)]
        table_warmer = keep.tile([P, 1], F32)
        nc.scalar.activation(out=table_warmer[:], in_=one_column[:], func=ACT.Exp)
        h_rows = h.rearrange("(p j) k -> p j k", j=ROWS)
        e_rows = embedding.rearrange("(p j) k -> p j k", j=ROWS)
        w2_raw = [keep.tile([P, HID], BF16, name="w2_raw%d" % i) for i in (0, 1)]
        h_pass = {}
        e_pass = {}
        h_pass[0] = load_group_pass(0, h_rows, 0, "h", 2)
        [wp1_pass] = load_weight(PRIOR, wp1, 2)
        nc.sync.dma_start(out=bias1[PRIOR][:], in_=bp1.rearrange("(p t) -> p t", p=P))
        nc.sync.dma_start(out=bias2_row[0:1, 0:DIST], in_=bp2.rearrange("(o d) -> o d", o=1))
        nc.sync.dma_start(
            out=bias2_row[0:1, DIST : 2 * DIST], in_=bq2.rearrange("(o d) -> o d", o=1)
        )
        h_pass[1] = load_group_pass(0, h_rows, 1, "h")
        h_pass[2] = load_group_pass(0, h_rows, 2, "h")
        e_pass[0] = load_group_pass(1, e_rows, 0, "e")
        wq1_pass = load_weight(POST, wq1, 1)
        nc.sync.dma_start(out=bias1[POST][:], in_=bq1.rearrange("(p t) -> p t", p=P))
        nc.sync.dma_start(out=w2_raw[PRIOR][:], in_=wp2)
        nc.sync.dma_start(out=w2_raw[POST][:], in_=wq2)
        for g in range(1, GROUPS):
            if g + PRIOR_AHEAD < GROUPS:
                h_pass[g + PRIOR_AHEAD] = load_group_pass(0, h_rows, g + PRIOR_AHEAD, "h")
            e_pass[g] = load_group_pass(1, e_rows, g, "e")
        arriving = {step - 2: [(h_pass, e_pass)[head][g]] for step, (g, head) in enumerate(steps)}
        arriving[0].append(e_pass[0])
        arriving[1] = wq1_pass

        grouped_of = {}
        banks_of = {}
        operand_of = {}

        def transpose_half(n, half):
            bank = psum_ring.tile([P, 2, 2 * P], F32, name="words_bank", tag="ring")
            for r in range(2):
                for u in range(2):
                    nc.tensor.transpose(
                        bank[:, u, r * P : (r + 1) * P],
                        pass_words[n][:, 2 * half + r, u * P : (u + 1) * P],
                        ident_f32[:],
                    )
            banks_of[n, half] = bank

        def transpose_pass(n):
            grouped_of[n] = stage.tile([P, GROUP, PACK], BF16, name="grouped", align_bytes=64)
            transpose_half(n, 0)
            transpose_half(n, 1)

        def scalar_empties(n, half):
            return half == 0 or (n >= 6 and n % 4 == 2)

        def empty_bank(n, half, by_scalar):
            out = grouped_of[n][:].bitcast(F32)[:, half * 2 * P : (half + 1) * 2 * P, :]
            in_ = banks_of[n, half][:].rearrange("p u c -> p c u")
            if by_scalar:
                nc.scalar.copy(out=out, in_=in_)
            else:
                nc.vector.tensor_copy(out=out, in_=in_)

        def quantise_pass(n, cols):
            if n in operand_of:
                codes, scales = operand_of[n]
            elif pass_weight[n] is None:
                name = pass_name[n]
                codes = quantised.tile([P, GROUP], U32, name=name + "_codes", align_bytes=64)[:]
                scales = quantised.tile([P, GROUP], U8, name=name + "_scales", align_bytes=64)[:]
            else:
                head, c = pass_weight[n]
                codes, scales = w1_codes[head][:, c, :], w1_scales[head][:, c, :]
            nc.vector.quantize_mx(
                out=codes[:, cols].bitcast(FP8X4),
                scales=scales[:, cols],
                in_=grouped_of[n][:, cols, :].rearrange("p c t -> p (c t)"),
            )
            operand_of[n] = (codes, scales)

        def first_layer_bank(step, t):
            g, head = steps[step]
            bank = psum_ring.tile([P, GROUP], F32, name="hidden_bank", tag="ring")
            units = slice(t * P, (t + 1) * P)
            passes = 1 + head
            for c in range(passes):
                codes, scales = operand_of[pass_of[(c, g)]]
                nc.tensor.matmul_mx(
                    out=bank[:],
                    lhsT=w1_codes[head][:, c, units].bitcast(FP8X4),
                    lhsT_scale=w1_scales[head][:, c, units],
                    rhs=codes.bitcast(FP8X4),
                    rhs_scale=scales,
                    start=(c == 0),
                    stop=(c == passes - 1),
                )
            return bank

        def relu_out(step, t, bank, hidden, cols):
            head = steps[step][1]
            nc.scalar.activation(
                out=hidden[:, t, cols],
                in_=bank[:, cols],
                func=ACT.Relu,
                bias=bias1[head][:, t : t + 1],
                scale=1.0,
            )

        w2_codes = [keep.tile([P, DIST], U32, name="w2_codes%d" % i, align_bytes=64) for i in (0, 1)]
        w2_scales = [keep.tile([P, DIST], U8, name="w2_scales%d" % i, align_bytes=64) for i in (0, 1)]
        bias2 = keep.tile([P, 2, DIST], F32)
        result = keep.tile([P, 2, 2, ROWS, STOC], F32)
        power = keep.tile([P, 2, ROWS, STOC], F32)
        mean_rows = [o.rearrange("(p j) d -> p j d", j=ROWS) for o in (out_2, out_0)]
        std_rows = [o.rearrange("(p j) d -> p j d", j=ROWS) for o in (out_3, out_1)]

        def regroup(hidden, grouped, cols):
            nc.vector.tensor_copy(
                out=grouped[:, cols, :].rearrange("p (c i) t -> p c t i", i=8),
                in_=hidden[:, :, cols].rearrange("p t (c i) -> p c t i", i=8),
            )

        def regroup_gpsimd(hidden, grouped, cols):
            nc.gpsimd.tensor_scalar(
                out=grouped[:, cols, :].rearrange("p (c i) t -> p c t i", i=8),
                in0=hidden[:, :, cols].rearrange("p t (c i) -> p c t i", i=8),
                scalar1=1.0,
                scalar2=0.0,
                op0=ALU.mult,
                op1=ALU.add,
            )

        def regroup_scalar(hidden, grouped, cols):
            nc.scalar.copy(
                out=grouped[:, cols, :].rearrange("p (c i) t -> p c t i", i=4),
                in_=hidden[:, :, cols].rearrange("p t (c i) -> p c t i", i=4),
            )

        def hidden_tiles():
            grouped = stage.tile([P, GROUP, PACK], BF16, name="hidden_grouped", align_bytes=64)
            codes = quantised.tile([P, GROUP], U32, name="hidden_codes", align_bytes=64)
            scales = quantised.tile([P, GROUP], U8, name="hidden_scales", align_bytes=64)
            return grouped, codes, scales

        def quantise_hidden(grouped, codes, scales, cols):
            nc.vector.quantize_mx(
                out=codes[:, cols].bitcast(FP8X4),
                scales=scales[:, cols],
                in_=grouped[:, cols, :].rearrange("p c t -> p (c t)"),
            )

        def second_layer(step, codes, scales, cols):
            g, head = steps[step]
            n_tiles = (cols.stop - cols.start) // P
            first_tile = g * TILES + cols.start // P
            tiles = slice(first_tile, first_tile + n_tiles)
            bank = psum_second.tile([P, n_tiles, DIST], F32, name="head_bank", tag="second")
            for j in range(n_tiles):
                rows = slice(cols.start + j * P, cols.start + (j + 1) * P)
                nc.tensor.matmul_mx(
                    out=bank[:, j, :],
                    lhsT=codes[:, rows].bitcast(FP8X4),
                    lhsT_scale=scales[:, rows],
                    rhs=w2_codes[head][:].bitcast(FP8X4),
                    rhs_scale=w2_scales[head][:],
                    start=True,
                    stop=True,
                )
            nc.vector.tensor_tensor(
                out=result[:, head, :, tiles, :].rearrange("p f j d -> p j f d"),
                in0=bank[:].rearrange("p j (f d) -> p j f d", f=2),
                in1=bias2[:, head, :]
                .rearrange("p (f d) -> p f d", f=2)
                .unsqueeze(1)
                .to_broadcast([P, n_tiles, 2, STOC]),
                op=ALU.add,
            )
            nc.sync.dma_start(out=mean_rows[head][:, tiles, :], in_=result[:, head, 0, tiles, :])

        def softplus_exp(g, heads=slice(0, 2)):
            tiles = slice(g * TILES, (g + 1) * TILES)
            nc.scalar.activation(
                out=power[:, heads, tiles, :], in_=result[:, heads, 1, tiles, :], func=ACT.Exp
            )

        def softplus_log(head, tiles):
            log_term = power[:, head, tiles, :]
            std = result[:, head, 1, tiles, :]
            nc.scalar.activation(out=log_term, in_=log_term, func=ACT.Ln, bias=math.exp(0.1))
            nc.vector.scalar_tensor_tensor(
                out=std, in0=log_term, scalar=LOG_CAP, in1=std, op0=ALU.min, op1=ALU.max
            )
            nc.sync.dma_start(out=std_rows[head][:, tiles, :], in_=std)

        def spread_bias2():
            bank = psum_second.tile([P, 2 * DIST], F32, name="bias2_bank", tag="second")
            nc.tensor.matmul(out=bank[:], lhsT=ones[:], rhs=bias2_row[:], start=True, stop=True)
            for f in range(2):
                nc.vector.tensor_scalar_add(
                    out=bias2[:, :, f * STOC : (f + 1) * STOC],
                    in0=bank[:].rearrange("p (h f d) -> p h f d", h=2, f=2)[:, :, f, :],
                    scalar1=0.1 * f,
                )

        w2_grouped = [
            keep.tile([P, DIST, PACK], BF16, name="w2_grouped%d" % i, align_bytes=64) for i in (0, 1)
        ]

        def transpose_w2(head):
            bank = psum_second.tile([P, CHUNKS, DIST], BF16, name="w2_bank", tag="second")
            for t in range(CHUNKS):
                nc.tensor.transpose(
                    bank[:, t, :], w2_raw[head][:, t:HID:CHUNKS], ident_bf16[:]
                )
            nc.scalar.copy(out=w2_grouped[head][:], in_=bank[:].rearrange("p t d -> p d t"))

        def quantise_w2(head):
            nc.vector.quantize_mx(
                out=w2_codes[head][:].bitcast(FP8X4),
                scales=w2_scales[head][:],
                in_=w2_grouped[head][:].rearrange("p d t -> p (d t)"),
            )

        whole = slice(0, GROUP)
        halves = [slice(0, GROUP // 2), slice(GROUP // 2, GROUP)]
        h0, h1 = h_pass[0], h_pass[1]
        transpose_pass(h0)
        empty_bank(h0, 0, True)
        empty_bank(h0, 1, False)
        transpose_pass(wp1_pass)
        empty_bank(wp1_pass, 0, True)
        quantise_pass(h0, whole)
        empty_bank(wp1_pass, 1, True)
        quantise_pass(wp1_pass, halves[0])
        quantise_pass(wp1_pass, halves[1])
        hidden_banks = [first_layer_bank(0, t) for t in (0, 1)]
        transpose_pass(h1)
        hidden_banks += [first_layer_bank(0, t) for t in (2, 3)]
        empty_bank(h1, 1, False)
        hidden_of = {0: stage.tile([P, CHUNKS, GROUP], BF16, name="hidden")}
        relu_out(0, 0, hidden_banks[0], hidden_of[0], whole)
        relu_out(0, 1, hidden_banks[1], hidden_of[0], whole)
        empty_bank(h1, 0, True)
        spread_bias2()

        n_steps = len(steps)
        tiles_of = {}
        for s in range(n_steps):
            here = arriving.get(s, [])
            for n in arriving.get(s - 1, []):
                quantise_pass(n, whole)
            if s == 2:
                quantise_w2(PRIOR)
                quantise_w2(POST)
            if s >= 1:
                tiles_of[s - 1] = hidden_tiles()
                g_cols = G_COLS if s > 2 else 0
                if g_cols:
                    regroup_gpsimd(hidden_of[s - 1], tiles_of[s - 1][0], slice(0, g_cols))
                regroup(hidden_of[s - 1], tiles_of[s - 1][0], slice(g_cols, GROUP))
            for n in here:
                transpose_pass(n)
            if s >= 2:
                second_layer(s - 2, *tiles_of[s - 2][1:], whole)
            for n in here:
                if not scalar_empties(n, 1):
                    empty_bank(n, 1, False)
            if s >= 1:
                quantise_hidden(*tiles_of[s - 1], whole)
            if s > 0:
                hidden_of[s] = stage.tile([P, CHUNKS, GROUP], BF16, name="hidden")
            if s + 1 < n_steps:
                next_banks = []
                for t in range(CHUNKS):
                    if s > 0 or t > 1:
                        relu_out(s, t, hidden_banks[t], hidden_of[s], whole)
                    next_banks.append(first_layer_bank(s + 1, t))
                hidden_banks = next_banks
            else:
                for cols in halves:
                    for t in range(CHUNKS):
                        relu_out(s, t, hidden_banks[t], hidden_of[s], cols)
            for n in here:
                empty_bank(n, 0, True)
                if scalar_empties(n, 1):
                    empty_bank(n, 1, True)
            if s == 1:
                transpose_w2(PRIOR)
                transpose_w2(POST)
            if s >= SOFTPLUS_LAG and steps[s - SOFTPLUS_LAG][1] == POST:
                softplus_exp(steps[s - SOFTPLUS_LAG][0])

        last = n_steps - 1
        tiles_of[last] = hidden_tiles()
        regroup(hidden_of[last], tiles_of[last][0], halves[0])
        second_layer(last - 1, *tiles_of[last - 1][1:], whole)
        quantise_hidden(*tiles_of[last], halves[0])
        regroup_scalar(hidden_of[last], tiles_of[last][0], halves[1])
        second_layer(last, *tiles_of[last][1:], halves[0])
        quantise_hidden(*tiles_of[last], halves[1])
        second_layer(last, *tiles_of[last][1:], halves[1])
        for g in range(GROUPS):
            if g < GROUPS - 1 and steps.index((g, POST)) + SOFTPLUS_LAG >= n_steps:
                softplus_exp(g)
        softplus_exp(GROUPS - 1, slice(PRIOR, PRIOR + 1))
        softplus_exp(GROUPS - 1, slice(POST, POST + 1))
        for head, pieces in ((PRIOR, (4, 8, 8, 12)), (POST, (12, 8, 8, 4))):
            first = 0
            for n_tiles in pieces:
                softplus_log(head, slice(first, first + n_tiles))
                first += n_tiles
